import numpy as np
import ml_dtypes


def mxq(x, axis, fmt="e4m3"):
    dtype, down = {"e4m3": (ml_dtypes.float8_e4m3fn, 7), "e5m2": (ml_dtypes.float8_e5m2, 14)}[fmt]
    v = np.moveaxis(np.asarray(x, np.float32).astype(ml_dtypes.bfloat16).astype(np.float64), axis, -1)
    blocks = v.reshape(v.shape[:-1] + (-1, 32))
    amax = np.abs(blocks).max(-1, keepdims=True)
    byte = np.maximum(np.where(amax > 0, np.frexp(amax)[1] - 1 + 127, 0) - down, 1)
    scale = np.exp2(byte - 127.0)
    codes = (blocks / scale).astype(np.float32).astype(dtype).astype(np.float64)
    return np.moveaxis((codes * scale).reshape(v.shape), -1, axis)


WIDE = False


def mx_kscale(k):
    if not WIDE:
        return np.ones(k)
    levels = np.array([10, -10, 5, -5, 0])
    if k % 512:
        return np.exp2(np.random.permutation(np.resize(levels, k // 32))).repeat(32)
    a = np.empty((k // 512, 16))
    for p in range(k // 512):
        a[p, :8] = np.random.permutation(np.resize(levels, 8))
        for g in range(8):
            far = levels[np.abs(levels - a[p, g]) >= 10]
            a[p, g + 8] = far[np.random.randint(len(far))]
    return np.exp2(a.ravel()).repeat(32)


BF16 = ml_dtypes.bfloat16


def bf(x):
    return np.asarray(x, np.float32).astype(BF16)


def f64(x):
    return np.asarray(x).astype(np.float64)


B, N, G, L = 256, 4096, 128, 768
N2 = 2 * N
L2 = 2 * L
L_LIMIT = 1.0


def relu(v):
    return np.maximum(v, 0.0)


def setup_inputs():
    s, t = mx_kscale(N2), mx_kscale(L2)
    return {
        "Volt": bf(np.random.standard_normal((B, N2)) * s),
        "IM": bf(np.random.standard_normal((L2, N2)) / np.sqrt(N2) / s[None, :] * t[:, None]),
        "Ybr": bf(np.random.standard_normal((L2, L2)) / np.sqrt(L2) / t[None, :]),
        "n_o_mu_i_u": bf(np.random.standard_normal((B, L))),
    }


def reference(Volt, IM, Ybr, n_o_mu_i_u):
    mu = f64(n_o_mu_i_u)
    dv = mxq(f64(Volt), 1, "e4m3") @ mxq(f64(IM), 1, "e4m3").T
    Ibr = mxq(dv, 1, "e4m3") @ mxq(f64(Ybr), 1, "e4m3").T
    i_up = Ibr[:, :L] ** 2 + Ibr[:, L:] ** 2 - L_LIMIT ** 2
    out = np.sum(relu(i_up), axis=1)
    out = out + np.sum(np.abs(mu * i_up), axis=1)
    out = out + np.sum(relu(-mu), axis=1)
    return out

@@ -1,0 +1,236 @@
+from contextlib import ExitStack
+
+import concourse.mybir as mybir
+from concourse.masks import make_identity
+
+F32 = mybir.dt.float32
+BF16 = mybir.dt.bfloat16
+U32 = mybir.dt.uint32
+U8 = mybir.dt.uint8
+FP8X4 = mybir.dt.float8_e4m3fn_x4
+ALU = mybir.AluOpType
+ACT = mybir.ActivationFunctionType
+
+P = 128
+PACK = 4
+K_PASS = P * PACK
+
+SAMPLES = 256
+VOLTS = 8192
+CURRENTS = 1536
+LINES = CURRENTS // 2
+LIMIT_SQUARED = 1.0
+
+PASSES_1 = VOLTS // K_PASS
+PASSES_2 = CURRENTS // K_PASS
+SAMPLE_TILES = SAMPLES // P
+
+BANK_COLS = 2 * P
+CHUNK_BANKS = 4
+CHUNK_K = 4096
+IM_TILES = CURRENTS // P
+IM_CHUNKS = VOLTS // CHUNK_K
+VOLT_CHUNKS = SAMPLES * VOLTS // (P * CHUNK_K)
+YBR_UNITS = CURRENTS // BANK_COLS
+FIRST_YBR_STEP = IM_TILES + 1 - YBR_UNITS
+LINE_TILES = LINES // BANK_COLS
+
+FLOPS = 2 * SAMPLES * CURRENTS * (VOLTS + CURRENTS)
+
+
+def tile_pinnlayer_pa_k_kernel(tc, Volt, IM, Ybr, n_o_mu_i_u, out):
+    nc = tc.nc
+    with ExitStack() as ctx:
+        keep = ctx.enter_context(tc.tile_pool(name="keep", bufs=1))
+        raw_pool = ctx.enter_context(tc.tile_pool(name="raw", bufs=8))
+        grouped_pool = ctx.enter_context(tc.tile_pool(name="grouped", bufs=3))
+        im_pool = ctx.enter_context(tc.tile_pool(name="im", bufs=3))
+        work = ctx.enter_context(tc.tile_pool(name="work", bufs=3))
+        bank_pool = ctx.enter_context(tc.psum_pool(name="bank", bufs=6))
+        acc_pool = ctx.enter_context(tc.psum_pool(name="acc", bufs=2))
+        ctx.enter_context(tc.manual_schedule())
+
+        identity = keep.tile([P, P], F32)
+        make_identity(nc, identity[:])
+
+        terms = keep.tile([P, SAMPLE_TILES, 2, 8], F32)
+        nc.vector.memset(terms[:], 0.0)
+        totals = keep.tile([P, P], F32)
+        nc.vector.memset(totals[:], 0.0)
+        table_warmer = keep.tile([P, 1], F32)
+        nc.scalar.activation(out=table_warmer[:], in_=totals[:, 0:1], func=ACT.Abs)
+
+        volt_codes = keep.tile([P, PASSES_1, SAMPLES], U32, align_bytes=64)
+        volt_scales = keep.tile([P, PASSES_1, SAMPLES], U8, align_bytes=64)
+        ybr_codes = keep.tile([P, YBR_UNITS, PASSES_2, BANK_COLS], U32, align_bytes=64)
+        ybr_scales = keep.tile([P, YBR_UNITS, PASSES_2, BANK_COLS], U8, align_bytes=64)
+        dv_grouped = keep.tile([P, PASSES_2, SAMPLES, PACK], BF16, align_bytes=64)
+        dv_codes = keep.tile([P, PASSES_2, SAMPLES], U32, align_bytes=64)
+        dv_scales = keep.tile([P, PASSES_2, SAMPLES], U8, align_bytes=64)
+        mu = keep.tile([P, SAMPLE_TILES, LINES], BF16)
+
+        def quantise(grouped, n_banks, codes, scales):
+            for bank in range(n_banks):
+                nc.vector.quantize_mx(
+                    out=codes[:, bank, :].bitcast(FP8X4),
+                    scales=scales[:, bank, :],
+                    in_=grouped[:, bank].rearrange("p s r t -> p (s r t)"),
+                )
+
+        def prepare(words, n_banks, codes, scales, chunk_before):
+            grouped = grouped_pool.tile([P, CHUNK_BANKS, 2, P, PACK], BF16, align_bytes=64)
+            for bank in range(n_banks):
+                flipped = bank_pool.tile([P, 2, 2, P], F32, tag="bank")
+                for s in range(2):
+                    for h in range(2):
+                        nc.tensor.transpose(flipped[:, s, h, :], words[:, bank, s, h, :], identity[:])
+                pairs_in = flipped[:].rearrange("p s h r -> p s r h")
+                pairs_out = grouped[:, bank].bitcast(F32)
+                if bank == n_banks - 1:
+                    nc.vector.tensor_copy(out=pairs_out, in_=pairs_in)
+                else:
+                    nc.scalar.copy(out=pairs_out, in_=pairs_in)
+            if chunk_before is not None:
+                quantise(*chunk_before)
+            return (grouped, n_banks, codes, scales)
+
+        volt_rows = Volt.rearrange("(s p) k -> p s k", p=P)
+        volt_chunk_k = CHUNK_K // SAMPLE_TILES
+        unquantised = None
+        for c in range(VOLT_CHUNKS):
+            raw = raw_pool.tile([P, SAMPLE_TILES, volt_chunk_k], BF16, tag="raw")
+            nc.sync.dma_start(out=raw[:], in_=volt_rows[:, :, c * volt_chunk_k : (c + 1) * volt_chunk_k])
+            passes = slice(c * CHUNK_BANKS, (c + 1) * CHUNK_BANKS)
+            unquantised = prepare(
+                raw[:].bitcast(F32).rearrange("p s (b w h) -> p b s h w", b=CHUNK_BANKS, h=2),
+                CHUNK_BANKS,
+                volt_codes[:, passes, :],
+                volt_scales[:, passes, :],
+                unquantised,
+            )
+
+        im_rows = IM.rearrange("(g p u e) k -> g u e p k", g=PASSES_2, u=2, p=P, e=2)
+        ybr_rows = Ybr.rearrange("(q s p) l -> q p s l", q=YBR_UNITS, s=2, p=P)
+
+        def first_matmul(g, u, e, acc, im_codes, im_scales):
+            for a in range(PASSES_1):
+                nc.tensor.matmul_mx(
+                    out=acc[:, e, :],
+                    lhsT=im_codes[:, a, :].bitcast(FP8X4),
+                    lhsT_scale=im_scales[:, a, :],
+                    rhs=volt_codes[:, a, :].bitcast(FP8X4),
+                    rhs_scale=volt_scales[:, a, :],
+                    start=(a == 0),
+                    stop=(a == PASSES_1 - 1),
+                )
+            if e == 1:
+                nc.vector.tensor_copy(
+                    out=dv_grouped[:, g, :, 2 * u : 2 * u + 2], in_=acc[:].rearrange("p e b -> p b e")
+                )
+            if e == 1 and u == 1:
+                nc.vector.quantize_mx(
+                    out=dv_codes[:, g, :].bitcast(FP8X4),
+                    scales=dv_scales[:, g, :],
+                    in_=dv_grouped[:, g].rearrange("p b t -> p (b t)"),
+                )
+
+        tile_before = None
+        acc = None
+        for step in range(IM_TILES + 1):
+            if step < IM_TILES:
+                g, u, e = step // 4, (step // 2) % 2, step % 2
+                im_codes = im_pool.tile([P, PASSES_1, P], U32, align_bytes=64)
+                im_scales = im_pool.tile([P, PASSES_1, P], U8, align_bytes=64)
+                for c in range(IM_CHUNKS):
+                    raw = raw_pool.tile([P, CHUNK_K], BF16, tag="raw")
+                    nc.sync.dma_start(out=raw[:], in_=im_rows[g, u, e, :, c * CHUNK_K : (c + 1) * CHUNK_K])
+                    passes = slice(c * 2 * CHUNK_BANKS, (c + 1) * 2 * CHUNK_BANKS)
+                    unquantised = prepare(
+                        raw[:].bitcast(F32).rearrange("p (b s w h) -> p b s h w", b=CHUNK_BANKS, s=2, h=2),
+                        CHUNK_BANKS,
+                        im_codes[:, passes, :].rearrange("p (b s) r -> p b (s r)", s=2),
+                        im_scales[:, passes, :].rearrange("p (b s) r -> p b (s r)", s=2),
+                        unquantised,
+                    )
+            else:
+                quantise(*unquantised)
+                unquantised = None
+                for t in range(SAMPLE_TILES):
+                    negative_part = work.tile([P, LINES], F32)
+                    nc.scalar.activation(
+                        out=negative_part[:], in_=mu[:, t, :], func=ACT.Relu, scale=-1.0,
+                        accum_out=terms[:, t, 0, LINE_TILES : LINE_TILES + 1],
+                    )
+            if tile_before is not None:
+                if tile_before[2] == 0:
+                    acc = acc_pool.tile([P, 2, SAMPLES], F32, tag="acc")
+                first_matmul(*tile_before[0:3], acc, *tile_before[3:5])
+            if step < IM_TILES:
+                tile_before = (g, u, e, im_codes, im_scales)
+            if step == FIRST_YBR_STEP:
+                nc.sync.dma_start(out=mu[:], in_=n_o_mu_i_u.rearrange("(t p) l -> p t l", p=P))
+            if step >= FIRST_YBR_STEP:
+                unit = step - FIRST_YBR_STEP
+                raw = raw_pool.tile([P, 2, CURRENTS], BF16, tag="raw")
+                nc.sync.dma_start(out=raw[:], in_=ybr_rows[unit])
+                unquantised = prepare(
+                    raw[:].bitcast(F32).rearrange("p s (b w h) -> p b s h w", b=PASSES_2, h=2),
+                    PASSES_2,
+                    ybr_codes[:, unit],
+                    ybr_scales[:, unit],
+                    unquantised,
+                )
+        quantise(*unquantised)
+
+        def sum_of_sizes(t, q, slack):
+            slack_size = work.tile([P, BANK_COLS], F32)
+            nc.scalar.activation(
+                out=slack_size[:], in_=slack[:], func=ACT.Abs, accum_out=terms[:, t, 0, q : q + 1]
+            )
+
+        bank_before = None
+        for q in range(LINE_TILES):
+            for t in range(SAMPLE_TILES):
+                samples = slice(t * P, (t + 1) * P)
+                ibr = bank_pool.tile([P, 2, BANK_COLS], F32, tag="bank")
+                for part in range(2):
+                    for g in range(PASSES_2):
+                        nc.tensor.matmul_mx(
+                            out=ibr[:, part, :],
+                            lhsT=dv_codes[:, g, samples].bitcast(FP8X4),
+                            lhsT_scale=dv_scales[:, g, samples],
+                            rhs=ybr_codes[:, part * LINE_TILES + q, g, :].bitcast(FP8X4),
+                            rhs_scale=ybr_scales[:, part * LINE_TILES + q, g, :],
+                            start=(g == 0),
+                            stop=(g == PASSES_2 - 1),
+                        )
+                squares = work.tile([P, 2, BANK_COLS], F32)
+                nc.scalar.activation(out=squares[:], in_=ibr[:], func=ACT.Square)
+                i_up = work.tile([P, BANK_COLS], F32)
+                nc.vector.scalar_tensor_tensor(
+                    out=i_up[:], in0=squares[:, 0, :], scalar=-LIMIT_SQUARED, in1=squares[:, 1, :],
+                    op0=ALU.add, op1=ALU.add,
+                )
+                slack = work.tile([P, BANK_COLS], F32)
+                nc.vector.tensor_tensor(
+                    out=slack[:], in0=i_up[:], in1=mu[:, t, q * BANK_COLS : (q + 1) * BANK_COLS], op=ALU.mult
+                )
+                excess = work.tile([P, BANK_COLS], F32)
+                nc.vector.tensor_scalar(
+                    out=excess[:], in0=i_up[:], scalar1=0.0, scalar2=None, op0=ALU.max, op1=ALU.add,
+                    accum_out=terms[:, t, 1, q : q + 1],
+                )
+                if bank_before is not None:
+                    sum_of_sizes(*bank_before)
+                bank_before = (t, q, slack)
+        sum_of_sizes(*bank_before)
+
+        nc.vector.tensor_reduce(
+            out=totals[:, 0:SAMPLE_TILES], in_=terms[:].rearrange("p t w c -> p t (w c)"),
+            axis=mybir.AxisListType.X, op=ALU.add,
+        )
+        totals_flipped = acc_pool.tile([P, P], F32, tag="acc")
+        nc.tensor.transpose(totals_flipped[:], totals[:], identity[:])
+        rows = keep.tile([P, P], F32)
+        nc.vector.tensor_copy(out=rows[:], in_=totals_flipped[:])
+        nc.sync.dma_start(out=out.rearrange("(t b) -> t b", t=SAMPLE_TILES), in_=rows[0:SAMPLE_TILES, :])

@@ -45,6 +45,7 @@ def tile_pinnlayer_pa_k_kernel(tc, Volt, IM, Ybr, n_o_mu_i_u, out):
         raw_pool = ctx.enter_context(tc.tile_pool(name="raw", bufs=8))
         grouped_pool = ctx.enter_context(tc.tile_pool(name="grouped", bufs=3))
         im_pool = ctx.enter_context(tc.tile_pool(name="im", bufs=3))
+        sorted_pool = ctx.enter_context(tc.tile_pool(name="sorted", bufs=3))
         work = ctx.enter_context(tc.tile_pool(name="work", bufs=3))
         bank_pool = ctx.enter_context(tc.psum_pool(name="bank", bufs=6))
         acc_pool = ctx.enter_context(tc.psum_pool(name="acc", bufs=2))
@@ -77,7 +78,7 @@ def tile_pinnlayer_pa_k_kernel(tc, Volt, IM, Ybr, n_o_mu_i_u, out):
                     in_=grouped[:, bank].rearrange("p s r t -> p (s r t)"),
                 )
 
-        def prepare(words, n_banks, codes, scales, chunk_before):
+        def prepare(words, n_banks, codes, scales, chunk_before, vector_copies=1):
             grouped = grouped_pool.tile([P, CHUNK_BANKS, 2, P, PACK], BF16, align_bytes=64)
             for bank in range(n_banks):
                 flipped = bank_pool.tile([P, 2, 2, P], F32, tag="bank")
@@ -86,7 +87,7 @@ def tile_pinnlayer_pa_k_kernel(tc, Volt, IM, Ybr, n_o_mu_i_u, out):
                         nc.tensor.transpose(flipped[:, s, h, :], words[:, bank, s, h, :], identity[:])
                 pairs_in = flipped[:].rearrange("p s h r -> p s r h")
                 pairs_out = grouped[:, bank].bitcast(F32)
-                if bank == n_banks - 1:
+                if bank >= n_banks - vector_copies:
                     nc.vector.tensor_copy(out=pairs_out, in_=pairs_in)
                 else:
                     nc.scalar.copy(out=pairs_out, in_=pairs_in)
@@ -134,23 +135,39 @@ def tile_pinnlayer_pa_k_kernel(tc, Volt, IM, Ybr, n_o_mu_i_u, out):
                     in_=dv_grouped[:, g].rearrange("p b t -> p (b t)"),
                 )
 
+        def load_and_sort(chunk):
+            tile, c = chunk // IM_CHUNKS, chunk % IM_CHUNKS
+            g, u, e = tile // 4, (tile // 2) % 2, tile % 2
+            raw = raw_pool.tile([P, CHUNK_K], BF16, tag="raw")
+            nc.sync.dma_start(out=raw[:], in_=im_rows[g, u, e, :, c * CHUNK_K : (c + 1) * CHUNK_K])
+            in_order = sorted_pool.tile([P, 2 * CHUNK_BANKS, 2, P], F32)
+            nc.vector.tensor_copy(
+                out=in_order[:],
+                in_=raw[:].bitcast(F32).rearrange("p (a w h) -> p a h w", a=2 * CHUNK_BANKS, h=2),
+            )
+            return in_order
+
         tile_before = None
         acc = None
+        in_order = load_and_sort(0)
         for step in range(IM_TILES + 1):
             if step < IM_TILES:
                 g, u, e = step // 4, (step // 2) % 2, step % 2
                 im_codes = im_pool.tile([P, PASSES_1, P], U32, align_bytes=64)
                 im_scales = im_pool.tile([P, PASSES_1, P], U8, align_bytes=64)
                 for c in range(IM_CHUNKS):
-                    raw = raw_pool.tile([P, CHUNK_K], BF16, tag="raw")
-                    nc.sync.dma_start(out=raw[:], in_=im_rows[g, u, e, :, c * CHUNK_K : (c + 1) * CHUNK_K])
+                    words = in_order[:].rearrange("p (b s) h w -> p b s h w", s=2)
+                    chunk_after = step * IM_CHUNKS + c + 1
+                    if chunk_after < IM_TILES * IM_CHUNKS:
+                        in_order = load_and_sort(chunk_after)
                     passes = slice(c * 2 * CHUNK_BANKS, (c + 1) * 2 * CHUNK_BANKS)
                     unquantised = prepare(
-                        raw[:].bitcast(F32).rearrange("p (b s w h) -> p b s h w", b=CHUNK_BANKS, s=2, h=2),
+                        words,
                         CHUNK_BANKS,
                         im_codes[:, passes, :].rearrange("p (b s) r -> p b (s r)", s=2),
                         im_scales[:, passes, :].rearrange("p (b s) r -> p b (s r)", s=2),
                         unquantised,
+                        vector_copies=0,
                     )
             else:
                 quantise(*unquantised)

@@ -14,6 +14,7 @@ ACT = mybir.ActivationFunctionType
 P = 128
 PACK = 4
 K_PASS = P * PACK
+RUN = 8
 
 SAMPLES = 256
 VOLTS = 8192
@@ -26,14 +27,20 @@ PASSES_2 = CURRENTS // K_PASS
 SAMPLE_TILES = SAMPLES // P
 
 BANK_COLS = 2 * P
-CHUNK_BANKS = 4
-CHUNK_K = 4096
+
+VOLT_CHUNK_PASSES = 2
+VOLT_CHUNKS = PASSES_1 // VOLT_CHUNK_PASSES
+IM_CHUNK_PASSES = 8
 IM_TILES = CURRENTS // P
-IM_CHUNKS = VOLTS // CHUNK_K
-VOLT_CHUNKS = SAMPLES * VOLTS // (P * CHUNK_K)
+IM_CHUNKS = PASSES_1 // IM_CHUNK_PASSES
 YBR_UNITS = CURRENTS // BANK_COLS
-FIRST_YBR_STEP = IM_TILES + 1 - YBR_UNITS
-LINE_TILES = LINES // BANK_COLS
+YBR_BANKS = YBR_UNITS * PASSES_2
+YBR_BANKS_A_STEP = 2
+FIRST_YBR_STEP = IM_TILES - YBR_BANKS // YBR_BANKS_A_STEP
+LINE_BLOCKS = LINES // BANK_COLS
+
+RAW_TILES = 7
+SORT_AHEAD = 2
 
 FLOPS = 2 * SAMPLES * CURRENTS * (VOLTS + CURRENTS)
 
@@ -42,11 +49,11 @@ def tile_pinnlayer_pa_k_kernel(tc, Volt, IM, Ybr, n_o_mu_i_u, out):
     nc = tc.nc
     with ExitStack() as ctx:
         keep = ctx.enter_context(tc.tile_pool(name="keep", bufs=1))
-        raw_pool = ctx.enter_context(tc.tile_pool(name="raw", bufs=8))
+        raw_pool = ctx.enter_context(tc.tile_pool(name="raw", bufs=RAW_TILES))
+        sorted_pool = ctx.enter_context(tc.tile_pool(name="sorted", bufs=SORT_AHEAD + 2))
         grouped_pool = ctx.enter_context(tc.tile_pool(name="grouped", bufs=3))
         im_pool = ctx.enter_context(tc.tile_pool(name="im", bufs=3))
-        sorted_pool = ctx.enter_context(tc.tile_pool(name="sorted", bufs=3))
-        work = ctx.enter_context(tc.tile_pool(name="work", bufs=3))
+        work = ctx.enter_context(tc.tile_pool(name="work", bufs=2))
         bank_pool = ctx.enter_context(tc.psum_pool(name="bank", bufs=6))
         acc_pool = ctx.enter_context(tc.psum_pool(name="acc", bufs=2))
         ctx.enter_context(tc.manual_schedule())
@@ -63,60 +70,126 @@ def tile_pinnlayer_pa_k_kernel(tc, Volt, IM, Ybr, n_o_mu_i_u, out):
 
         volt_codes = keep.tile([P, PASSES_1, SAMPLES], U32, align_bytes=64)
         volt_scales = keep.tile([P, PASSES_1, SAMPLES], U8, align_bytes=64)
-        ybr_codes = keep.tile([P, YBR_UNITS, PASSES_2, BANK_COLS], U32, align_bytes=64)
-        ybr_scales = keep.tile([P, YBR_UNITS, PASSES_2, BANK_COLS], U8, align_bytes=64)
+        ybr_codes = keep.tile([P, PASSES_2, LINE_BLOCKS, 2, BANK_COLS], U32, align_bytes=64)
+        ybr_scales = keep.tile([P, PASSES_2, LINE_BLOCKS, 2, BANK_COLS], U8, align_bytes=64)
         dv_grouped = keep.tile([P, PASSES_2, SAMPLES, PACK], BF16, align_bytes=64)
         dv_codes = keep.tile([P, PASSES_2, SAMPLES], U32, align_bytes=64)
         dv_scales = keep.tile([P, PASSES_2, SAMPLES], U8, align_bytes=64)
         mu = keep.tile([P, SAMPLE_TILES, LINES], BF16)
+        mu_size = keep.tile([P, SAMPLE_TILES, LINES], F32)
+        weight = keep.tile([P, SAMPLE_TILES, LINES], F32)
 
-        def quantise(grouped, n_banks, codes, scales):
-            for bank in range(n_banks):
-                nc.vector.quantize_mx(
-                    out=codes[:, bank, :].bitcast(FP8X4),
-                    scales=scales[:, bank, :],
-                    in_=grouped[:, bank].rearrange("p s r t -> p (s r t)"),
-                )
+        volt_rows = Volt.rearrange("(s p) k -> p s k", p=P)
+        im_rows = IM.rearrange("(g p t) k -> g t p k", g=PASSES_2, p=P, t=PACK)
+        ybr_rows = Ybr.rearrange("(n s p) l -> n p s l", n=YBR_UNITS, s=2, p=P)
+        volt_chunk_k = VOLT_CHUNK_PASSES * K_PASS
+        im_chunk_k = IM_CHUNK_PASSES * K_PASS
 
-        def prepare(words, n_banks, codes, scales, chunk_before, vector_copies=1):
-            grouped = grouped_pool.tile([P, CHUNK_BANKS, 2, P, PACK], BF16, align_bytes=64)
+        load_order = [("volt", c) for c in range(VOLT_CHUNKS)]
+        for chunk in range(IM_TILES * IM_CHUNKS):
+            load_order.append(("im", chunk))
+            for unit in range(YBR_UNITS):
+                first_step = FIRST_YBR_STEP + unit * PASSES_2 // YBR_BANKS_A_STEP
+                if chunk == (first_step - 1) * IM_CHUNKS + 1:
+                    load_order.append(("ybr", unit))
+        raw = {}
+
+        def load_next():
+            if not load_order:
+                return
+            kind, n = load_order[0]
+            load_order.remove(load_order[0])
+            if kind == "volt":
+                tile = raw_pool.tile([P, SAMPLE_TILES, volt_chunk_k], BF16, tag="raw")
+                source = volt_rows[:, :, n * volt_chunk_k : (n + 1) * volt_chunk_k]
+            elif kind == "im":
+                tile = raw_pool.tile([P, im_chunk_k], BF16, tag="raw")
+                t, c = n // IM_CHUNKS, n % IM_CHUNKS
+                source = im_rows[t // PACK, t % PACK, :, c * im_chunk_k : (c + 1) * im_chunk_k]
+            else:
+                tile = raw_pool.tile([P, 2, CURRENTS], BF16, tag="raw")
+                source = ybr_rows[n]
+            nc.sync.dma_start(out=tile[:], in_=source)
+            raw[(kind, n)] = tile
+
+        def sort_words(kind, n, sets):
+            tile = raw[(kind, n)]
+            tile_in_order = sorted_pool.tile([P, sets, 2, P], F32, tag="sorted")
+            flat = tile[:].rearrange("p s k -> p (s k)") if kind == "volt" else tile[:]
+            nc.vector.tensor_copy(
+                out=tile_in_order[:].rearrange("p a h (m j) -> p a h m j", j=RUN),
+                in_=flat.bitcast(F32).rearrange("p (a m h j) -> p a h m j", a=sets, h=2, j=RUN),
+            )
+            load_next()
+            return tile_in_order
+
+        def transpose_banks(words, n_banks, tag):
+            grouped = grouped_pool.tile([P, n_banks, 2 * P * PACK], BF16, tag=tag, align_bytes=64)
             for bank in range(n_banks):
                 flipped = bank_pool.tile([P, 2, 2, P], F32, tag="bank")
                 for s in range(2):
                     for h in range(2):
                         nc.tensor.transpose(flipped[:, s, h, :], words[:, bank, s, h, :], identity[:])
-                pairs_in = flipped[:].rearrange("p s h r -> p s r h")
-                pairs_out = grouped[:, bank].bitcast(F32)
-                if bank >= n_banks - vector_copies:
-                    nc.vector.tensor_copy(out=pairs_out, in_=pairs_in)
-                else:
-                    nc.scalar.copy(out=pairs_out, in_=pairs_in)
-            if chunk_before is not None:
-                quantise(*chunk_before)
-            return (grouped, n_banks, codes, scales)
+                nc.scalar.copy(
+                    out=grouped[:, bank, :].bitcast(F32).rearrange("p (s r h) -> p s r h", s=2, h=2),
+                    in_=flipped[:].rearrange("p s h r -> p s r h"),
+                )
+            return grouped
 
-        volt_rows = Volt.rearrange("(s p) k -> p s k", p=P)
-        volt_chunk_k = CHUNK_K // SAMPLE_TILES
-        unquantised = None
+        def quantise(grouped, codes, scales):
+            nc.vector.quantize_mx(out=codes.bitcast(FP8X4), scales=scales, in_=grouped)
+
+        for load in range(RAW_TILES):
+            load_next()
+
+        waiting = []
+
+        def quantise_waiting():
+            for operands in waiting:
+                quantise(*operands)
+            waiting.clear()
+
+        sort_order = [("volt", c, SAMPLE_TILES * VOLT_CHUNK_PASSES) for c in range(VOLT_CHUNKS)]
+        sort_order.extend([("im", chunk, IM_CHUNK_PASSES) for chunk in range(IM_TILES * IM_CHUNKS)])
+        in_order = {}
+
+        def sort_next():
+            if sort_order:
+                kind, n, sets = sort_order[0]
+                sort_order.remove(sort_order[0])
+                in_order[(kind, n)] = sort_words(kind, n, sets)
+
+        for chunk in range(SORT_AHEAD):
+            sort_next()
+
         for c in range(VOLT_CHUNKS):
-            raw = raw_pool.tile([P, SAMPLE_TILES, volt_chunk_k], BF16, tag="raw")
-            nc.sync.dma_start(out=raw[:], in_=volt_rows[:, :, c * volt_chunk_k : (c + 1) * volt_chunk_k])
-            passes = slice(c * CHUNK_BANKS, (c + 1) * CHUNK_BANKS)
-            unquantised = prepare(
-                raw[:].bitcast(F32).rearrange("p s (b w h) -> p b s h w", b=CHUNK_BANKS, h=2),
-                CHUNK_BANKS,
-                volt_codes[:, passes, :],
-                volt_scales[:, passes, :],
-                unquantised,
+            sort_next()
+            grouped = transpose_banks(
+                in_order[("volt", c)][:].rearrange("p (s b) h w -> p b s h w", s=SAMPLE_TILES),
+                VOLT_CHUNK_PASSES,
+                "chunk",
+            )
+            quantise_waiting()
+            passes = slice(c * VOLT_CHUNK_PASSES, (c + 1) * VOLT_CHUNK_PASSES)
+            waiting.append(
+                (
+                    grouped[:].rearrange("p b v -> p (b v)"),
+                    volt_codes[:, passes, :].rearrange("p a r -> p (a r)"),
+                    volt_scales[:, passes, :].rearrange("p a r -> p (a r)"),
+                )
             )
 
-        im_rows = IM.rearrange("(g p u e) k -> g u e p k", g=PASSES_2, u=2, p=P, e=2)
-        ybr_rows = Ybr.rearrange("(q s p) l -> q p s l", q=YBR_UNITS, s=2, p=P)
+        acc_tiles = {}
+        im_tiles = {}
 
-        def first_matmul(g, u, e, acc, im_codes, im_scales):
-            for a in range(PASSES_1):
+        def first_matmul(t, passes):
+            im_codes, im_scales = im_tiles[t]
+            pair, e = t // 2, t % 2
+            if pair not in acc_tiles:
+                acc_tiles[pair] = acc_pool.tile([P, 2, SAMPLES], F32, tag="acc", name="acc")
+            for a in passes:
                 nc.tensor.matmul_mx(
-                    out=acc[:, e, :],
+                    out=acc_tiles[pair][:, e, :],
                     lhsT=im_codes[:, a, :].bitcast(FP8X4),
                     lhsT_scale=im_scales[:, a, :],
                     rhs=volt_codes[:, a, :].bitcast(FP8X4),
@@ -124,123 +197,115 @@ def tile_pinnlayer_pa_k_kernel(tc, Volt, IM, Ybr, n_o_mu_i_u, out):
                     start=(a == 0),
                     stop=(a == PASSES_1 - 1),
                 )
-            if e == 1:
-                nc.vector.tensor_copy(
-                    out=dv_grouped[:, g, :, 2 * u : 2 * u + 2], in_=acc[:].rearrange("p e b -> p b e")
-                )
-            if e == 1 and u == 1:
-                nc.vector.quantize_mx(
-                    out=dv_codes[:, g, :].bitcast(FP8X4),
-                    scales=dv_scales[:, g, :],
-                    in_=dv_grouped[:, g].rearrange("p b t -> p (b t)"),
-                )
 
-        def load_and_sort(chunk):
-            tile, c = chunk // IM_CHUNKS, chunk % IM_CHUNKS
-            g, u, e = tile // 4, (tile // 2) % 2, tile % 2
-            raw = raw_pool.tile([P, CHUNK_K], BF16, tag="raw")
-            nc.sync.dma_start(out=raw[:], in_=im_rows[g, u, e, :, c * CHUNK_K : (c + 1) * CHUNK_K])
-            in_order = sorted_pool.tile([P, 2 * CHUNK_BANKS, 2, P], F32)
+        def round_dv(pair):
+            g, u = pair // 2, pair % 2
             nc.vector.tensor_copy(
-                out=in_order[:],
-                in_=raw[:].bitcast(F32).rearrange("p (a w h) -> p a h w", a=2 * CHUNK_BANKS, h=2),
+                out=dv_grouped[:, g, :, 2 * u : 2 * u + 2],
+                in_=acc_tiles[pair][:].rearrange("p e b -> p b e"),
             )
-            return in_order
+            if u == 1:
+                quantise(dv_grouped[:, g].rearrange("p b t -> p (b t)"), dv_codes[:, g, :], dv_scales[:, g, :])
 
-        tile_before = None
-        acc = None
-        in_order = load_and_sort(0)
-        for step in range(IM_TILES + 1):
-            if step < IM_TILES:
-                g, u, e = step // 4, (step // 2) % 2, step % 2
-                im_codes = im_pool.tile([P, PASSES_1, P], U32, align_bytes=64)
-                im_scales = im_pool.tile([P, PASSES_1, P], U8, align_bytes=64)
-                for c in range(IM_CHUNKS):
-                    words = in_order[:].rearrange("p (b s) h w -> p b s h w", s=2)
-                    chunk_after = step * IM_CHUNKS + c + 1
-                    if chunk_after < IM_TILES * IM_CHUNKS:
-                        in_order = load_and_sort(chunk_after)
-                    passes = slice(c * 2 * CHUNK_BANKS, (c + 1) * 2 * CHUNK_BANKS)
-                    unquantised = prepare(
-                        words,
-                        CHUNK_BANKS,
-                        im_codes[:, passes, :].rearrange("p (b s) r -> p b (s r)", s=2),
-                        im_scales[:, passes, :].rearrange("p (b s) r -> p b (s r)", s=2),
-                        unquantised,
-                        vector_copies=0,
+        def ybr_banks(first, n_banks):
+            for bank in range(first, first + n_banks):
+                unit, g = bank // PASSES_2, bank % PASSES_2
+                words = raw[("ybr", unit)][:].bitcast(F32).rearrange("p s (g w h) -> p g s h w", g=PASSES_2, h=2)
+                grouped = transpose_banks(words[:, g : g + 1], 1, "ybr")
+                part, q = unit // LINE_BLOCKS, unit % LINE_BLOCKS
+                waiting.append((grouped[:, 0, :], ybr_codes[:, g, q, part, :], ybr_scales[:, g, q, part, :]))
+                if g == PASSES_2 - 1:
+                    load_next()
+
+        for t in range(IM_TILES):
+            im_codes = im_pool.tile([P, PASSES_1, P], U32, align_bytes=64)
+            im_scales = im_pool.tile([P, PASSES_1, P], U8, align_bytes=64)
+            im_tiles[t] = (im_codes, im_scales)
+            for c in range(IM_CHUNKS):
+                chunk = t * IM_CHUNKS + c
+                quantise_waiting()
+                sort_next()
+                grouped = transpose_banks(
+                    in_order[("im", chunk)][:].rearrange("p (b s) h w -> p b s h w", s=2), IM_CHUNK_PASSES // 2, "chunk"
+                )
+                passes = slice(c * IM_CHUNK_PASSES, (c + 1) * IM_CHUNK_PASSES)
+                waiting.append(
+                    (
+                        grouped[:].rearrange("p b v -> p (b v)"),
+                        im_codes[:, passes, :].rearrange("p a r -> p (a r)"),
+                        im_scales[:, passes, :].rearrange("p a r -> p (a r)"),
                     )
-            else:
-                quantise(*unquantised)
-                unquantised = None
-                for t in range(SAMPLE_TILES):
+                )
+                if c == 0 and t >= 3 and t % 2 == 1:
+                    round_dv((t - 3) // 2)
+            if t >= FIRST_YBR_STEP:
+                ybr_banks((t - FIRST_YBR_STEP) * YBR_BANKS_A_STEP, YBR_BANKS_A_STEP)
+            if t == FIRST_YBR_STEP:
+                nc.sync.dma_start(out=mu[:], in_=n_o_mu_i_u.rearrange("(t p) l -> p t l", p=P))
+            if t == FIRST_YBR_STEP + 2:
+                for s in range(SAMPLE_TILES):
                     negative_part = work.tile([P, LINES], F32)
                     nc.scalar.activation(
-                        out=negative_part[:], in_=mu[:, t, :], func=ACT.Relu, scale=-1.0,
-                        accum_out=terms[:, t, 0, LINE_TILES : LINE_TILES + 1],
+                        out=negative_part[:], in_=mu[:, s, :], func=ACT.Relu, scale=-2.0,
+                        accum_out=terms[:, s, 0, LINE_BLOCKS : LINE_BLOCKS + 1],
                     )
-            if tile_before is not None:
-                if tile_before[2] == 0:
-                    acc = acc_pool.tile([P, 2, SAMPLES], F32, tag="acc")
-                first_matmul(*tile_before[0:3], acc, *tile_before[3:5])
-            if step < IM_TILES:
-                tile_before = (g, u, e, im_codes, im_scales)
-            if step == FIRST_YBR_STEP:
-                nc.sync.dma_start(out=mu[:], in_=n_o_mu_i_u.rearrange("(t p) l -> p t l", p=P))
-            if step >= FIRST_YBR_STEP:
-                unit = step - FIRST_YBR_STEP
-                raw = raw_pool.tile([P, 2, CURRENTS], BF16, tag="raw")
-                nc.sync.dma_start(out=raw[:], in_=ybr_rows[unit])
-                unquantised = prepare(
-                    raw[:].bitcast(F32).rearrange("p s (b w h) -> p b s h w", b=PASSES_2, h=2),
-                    PASSES_2,
-                    ybr_codes[:, unit],
-                    ybr_scales[:, unit],
-                    unquantised,
-                )
-        quantise(*unquantised)
+                    nc.scalar.activation(out=mu_size[:, s, :], in_=mu[:, s, :], func=ACT.Abs)
+                    nc.gpsimd.tensor_scalar(
+                        out=weight[:, s, :], in0=mu_size[:, s, :], scalar1=2.0, scalar2=1.0,
+                        op0=ALU.mult, op1=ALU.add,
+                    )
+            if t >= 1:
+                first_matmul(t - 1, range(PASSES_1))
 
-        def sum_of_sizes(t, q, slack):
-            slack_size = work.tile([P, BANK_COLS], F32)
-            nc.scalar.activation(
-                out=slack_size[:], in_=slack[:], func=ACT.Abs, accum_out=terms[:, t, 0, q : q + 1]
+        quantise_waiting()
+        ibr = {}
+
+        def second_matmul(q, t, passes):
+            samples = slice(t * P, (t + 1) * P)
+            for g in passes:
+                nc.tensor.matmul_mx(
+                    out=ibr[(q, t)][:],
+                    lhsT=dv_codes[:, g, samples].bitcast(FP8X4),
+                    lhsT_scale=dv_scales[:, g, samples],
+                    rhs=ybr_codes[:, g, q].rearrange("p c n -> p (c n)").bitcast(FP8X4),
+                    rhs_scale=ybr_scales[:, g, q].rearrange("p c n -> p (c n)"),
+                    start=(g == 0),
+                    stop=(g == PASSES_2 - 1),
+                )
+
+        blocks = [(q, t) for q in range(LINE_BLOCKS) for t in range(SAMPLE_TILES)]
+        first_matmul(IM_TILES - 1, range(PASSES_1))
+        for q, t in blocks:
+            ibr[(q, t)] = bank_pool.tile([P, 2 * BANK_COLS], F32, tag="bank", name="ibr")
+            second_matmul(q, t, range(PASSES_2 - 1))
+        round_dv(IM_TILES // 2 - 1)
+
+        def weighted_sum(q, t, i_up):
+            i_size = work.tile([P, BANK_COLS], F32)
+            nc.scalar.activation(out=i_size[:], in_=i_up[:], func=ACT.Abs)
+            weighted = work.tile([P, BANK_COLS], F32)
+            nc.vector.scalar_tensor_tensor(
+                out=weighted[:], in0=i_size[:], scalar=1.0, in1=weight[:, t, q * BANK_COLS : (q + 1) * BANK_COLS],
+                op0=ALU.mult, op1=ALU.mult, accum_out=terms[:, t, 1, q : q + 1],
             )
 
-        bank_before = None
-        for q in range(LINE_TILES):
-            for t in range(SAMPLE_TILES):
-                samples = slice(t * P, (t + 1) * P)
-                ibr = bank_pool.tile([P, 2, BANK_COLS], F32, tag="bank")
-                for part in range(2):
-                    for g in range(PASSES_2):
-                        nc.tensor.matmul_mx(
-                            out=ibr[:, part, :],
-                            lhsT=dv_codes[:, g, samples].bitcast(FP8X4),
-                            lhsT_scale=dv_scales[:, g, samples],
-                            rhs=ybr_codes[:, part * LINE_TILES + q, g, :].bitcast(FP8X4),
-                            rhs_scale=ybr_scales[:, part * LINE_TILES + q, g, :],
-                            start=(g == 0),
-                            stop=(g == PASSES_2 - 1),
-                        )
-                squares = work.tile([P, 2, BANK_COLS], F32)
-                nc.scalar.activation(out=squares[:], in_=ibr[:], func=ACT.Square)
-                i_up = work.tile([P, BANK_COLS], F32)
-                nc.vector.scalar_tensor_tensor(
-                    out=i_up[:], in0=squares[:, 0, :], scalar=-LIMIT_SQUARED, in1=squares[:, 1, :],
-                    op0=ALU.add, op1=ALU.add,
-                )
-                slack = work.tile([P, BANK_COLS], F32)
-                nc.vector.tensor_tensor(
-                    out=slack[:], in0=i_up[:], in1=mu[:, t, q * BANK_COLS : (q + 1) * BANK_COLS], op=ALU.mult
-                )
-                excess = work.tile([P, BANK_COLS], F32)
-                nc.vector.tensor_scalar(
-                    out=excess[:], in0=i_up[:], scalar1=0.0, scalar2=None, op0=ALU.max, op1=ALU.add,
-                    accum_out=terms[:, t, 1, q : q + 1],
-                )
-                if bank_before is not None:
-                    sum_of_sizes(*bank_before)
-                bank_before = (t, q, slack)
-        sum_of_sizes(*bank_before)
+        block_before = None
+        for q, t in blocks:
+            second_matmul(q, t, range(PASSES_2 - 1, PASSES_2))
+            squares = work.tile([P, 2, BANK_COLS], F32)
+            nc.scalar.activation(
+                out=squares[:].rearrange("p c n -> p (c n)"), in_=ibr[(q, t)][:], func=ACT.Square,
+                accum_out=terms[:, t, 0, q : q + 1],
+            )
+            i_up = work.tile([P, BANK_COLS], F32)
+            nc.vector.scalar_tensor_tensor(
+                out=i_up[:], in0=squares[:, 0, :], scalar=-LIMIT_SQUARED, in1=squares[:, 1, :],
+                op0=ALU.add, op1=ALU.add,
+            )
+            if block_before is not None:
+                weighted_sum(*block_before)
+            block_before = (q, t, i_up)
+        weighted_sum(*block_before)
 
         nc.vector.tensor_reduce(
             out=totals[:, 0:SAMPLE_TILES], in_=terms[:].rearrange("p t w c -> p t (w c)"),
@@ -249,5 +314,8 @@ def tile_pinnlayer_pa_k_kernel(tc, Volt, IM, Ybr, n_o_mu_i_u, out):
         totals_flipped = acc_pool.tile([P, P], F32, tag="acc")
         nc.tensor.transpose(totals_flipped[:], totals[:], identity[:])
         rows = keep.tile([P, P], F32)
-        nc.vector.tensor_copy(out=rows[:], in_=totals_flipped[:])
+        nc.vector.tensor_scalar(
+            out=rows[:], in0=totals_flipped[:], scalar1=0.5, scalar2=-0.5 * LINES * LIMIT_SQUARED,
+            op0=ALU.mult, op1=ALU.add,
+        )
         nc.sync.dma_start(out=out.rearrange("(t b) -> t b", t=SAMPLE_TILES), in_=rows[0:SAMPLE_TILES, :])

@@ -34,13 +34,13 @@ IM_CHUNK_PASSES = 8
 IM_TILES = CURRENTS // P
 IM_CHUNKS = PASSES_1 // IM_CHUNK_PASSES
 YBR_UNITS = CURRENTS // BANK_COLS
-YBR_BANKS = YBR_UNITS * PASSES_2
-YBR_BANKS_A_STEP = 2
-FIRST_YBR_STEP = IM_TILES - YBR_BANKS // YBR_BANKS_A_STEP
+FIRST_YBR_STEP = IM_TILES - YBR_UNITS
 LINE_BLOCKS = LINES // BANK_COLS
 
 RAW_TILES = 7
 SORT_AHEAD = 2
+
+EARLY_BLOCKS = 3
 
 FLOPS = 2 * SAMPLES * CURRENTS * (VOLTS + CURRENTS)
 
@@ -52,7 +52,7 @@ def tile_pinnlayer_pa_k_kernel(tc, Volt, IM, Ybr, n_o_mu_i_u, out):
         raw_pool = ctx.enter_context(tc.tile_pool(name="raw", bufs=RAW_TILES))
         sorted_pool = ctx.enter_context(tc.tile_pool(name="sorted", bufs=SORT_AHEAD + 2))
         grouped_pool = ctx.enter_context(tc.tile_pool(name="grouped", bufs=3))
-        im_pool = ctx.enter_context(tc.tile_pool(name="im", bufs=3))
+        im_pool = ctx.enter_context(tc.tile_pool(name="im", bufs=2))
         work = ctx.enter_context(tc.tile_pool(name="work", bufs=2))
         bank_pool = ctx.enter_context(tc.psum_pool(name="bank", bufs=6))
         acc_pool = ctx.enter_context(tc.psum_pool(name="acc", bufs=2))
@@ -76,7 +76,6 @@ def tile_pinnlayer_pa_k_kernel(tc, Volt, IM, Ybr, n_o_mu_i_u, out):
         dv_codes = keep.tile([P, PASSES_2, SAMPLES], U32, align_bytes=64)
         dv_scales = keep.tile([P, PASSES_2, SAMPLES], U8, align_bytes=64)
         mu = keep.tile([P, SAMPLE_TILES, LINES], BF16)
-        mu_size = keep.tile([P, SAMPLE_TILES, LINES], F32)
         weight = keep.tile([P, SAMPLE_TILES, LINES], F32)
 
         volt_rows = Volt.rearrange("(s p) k -> p s k", p=P)
@@ -86,19 +85,14 @@ def tile_pinnlayer_pa_k_kernel(tc, Volt, IM, Ybr, n_o_mu_i_u, out):
         im_chunk_k = IM_CHUNK_PASSES * K_PASS
 
         load_order = [("volt", c) for c in range(VOLT_CHUNKS)]
-        for chunk in range(IM_TILES * IM_CHUNKS):
-            load_order.append(("im", chunk))
-            for unit in range(YBR_UNITS):
-                first_step = FIRST_YBR_STEP + unit * PASSES_2 // YBR_BANKS_A_STEP
-                if chunk == (first_step - 1) * IM_CHUNKS + 1:
-                    load_order.append(("ybr", unit))
+        for t in range(IM_TILES):
+            load_order.extend([("im", t * IM_CHUNKS + c) for c in range(IM_CHUNKS)])
+            if 0 <= t - FIRST_YBR_STEP < YBR_UNITS:
+                load_order.append(("ybr", t - FIRST_YBR_STEP))
+        used = {}
         raw = {}
 
-        def load_next():
-            if not load_order:
-                return
-            kind, n = load_order[0]
-            load_order.remove(load_order[0])
+        def load(kind, n):
             if kind == "volt":
                 tile = raw_pool.tile([P, SAMPLE_TILES, volt_chunk_k], BF16, tag="raw")
                 source = volt_rows[:, :, n * volt_chunk_k : (n + 1) * volt_chunk_k]
@@ -112,6 +106,11 @@ def tile_pinnlayer_pa_k_kernel(tc, Volt, IM, Ybr, n_o_mu_i_u, out):
             nc.sync.dma_start(out=tile[:], in_=source)
             raw[(kind, n)] = tile
 
+        def mark_used(kind, n):
+            used[(kind, n)] = True
+            while len(raw) < len(load_order) and load_order[len(raw) - RAW_TILES] in used:
+                load(*load_order[len(raw)])
+
         def sort_words(kind, n, sets):
             tile = raw[(kind, n)]
             tile_in_order = sorted_pool.tile([P, sets, 2, P], F32, tag="sorted")
@@ -120,11 +119,11 @@ def tile_pinnlayer_pa_k_kernel(tc, Volt, IM, Ybr, n_o_mu_i_u, out):
                 out=tile_in_order[:].rearrange("p a h (m j) -> p a h m j", j=RUN),
                 in_=flat.bitcast(F32).rearrange("p (a m h j) -> p a h m j", a=sets, h=2, j=RUN),
             )
-            load_next()
+            mark_used(kind, n)
             return tile_in_order
 
-        def transpose_banks(words, n_banks, tag):
-            grouped = grouped_pool.tile([P, n_banks, 2 * P * PACK], BF16, tag=tag, align_bytes=64)
+        def transpose_banks(words, n_banks):
+            grouped = grouped_pool.tile([P, n_banks, 2 * P * PACK], BF16, tag="grouped", align_bytes=64)
             for bank in range(n_banks):
                 flipped = bank_pool.tile([P, 2, 2, P], F32, tag="bank")
                 for s in range(2):
@@ -139,8 +138,8 @@ def tile_pinnlayer_pa_k_kernel(tc, Volt, IM, Ybr, n_o_mu_i_u, out):
         def quantise(grouped, codes, scales):
             nc.vector.quantize_mx(out=codes.bitcast(FP8X4), scales=scales, in_=grouped)
 
-        for load in range(RAW_TILES):
-            load_next()
+        for item in load_order[:RAW_TILES]:
+            load(*item)
 
         waiting = []
 
@@ -165,9 +164,7 @@ def tile_pinnlayer_pa_k_kernel(tc, Volt, IM, Ybr, n_o_mu_i_u, out):
         for c in range(VOLT_CHUNKS):
             sort_next()
             grouped = transpose_banks(
-                in_order[("volt", c)][:].rearrange("p (s b) h w -> p b s h w", s=SAMPLE_TILES),
-                VOLT_CHUNK_PASSES,
-                "chunk",
+                in_order[("volt", c)][:].rearrange("p (s b) h w -> p b s h w", s=SAMPLE_TILES), VOLT_CHUNK_PASSES
             )
             quantise_waiting()
             passes = slice(c * VOLT_CHUNK_PASSES, (c + 1) * VOLT_CHUNK_PASSES)
@@ -207,15 +204,13 @@ def tile_pinnlayer_pa_k_kernel(tc, Volt, IM, Ybr, n_o_mu_i_u, out):
             if u == 1:
                 quantise(dv_grouped[:, g].rearrange("p b t -> p (b t)"), dv_codes[:, g, :], dv_scales[:, g, :])
 
-        def ybr_banks(first, n_banks):
-            for bank in range(first, first + n_banks):
-                unit, g = bank // PASSES_2, bank % PASSES_2
-                words = raw[("ybr", unit)][:].bitcast(F32).rearrange("p s (g w h) -> p g s h w", g=PASSES_2, h=2)
-                grouped = transpose_banks(words[:, g : g + 1], 1, "ybr")
-                part, q = unit // LINE_BLOCKS, unit % LINE_BLOCKS
-                waiting.append((grouped[:, 0, :], ybr_codes[:, g, q, part, :], ybr_scales[:, g, q, part, :]))
-                if g == PASSES_2 - 1:
-                    load_next()
+        def transpose_ybr(unit):
+            words = raw[("ybr", unit)][:].bitcast(F32).rearrange("p s (g w h) -> p g s h w", g=PASSES_2, h=2)
+            grouped = transpose_banks(words, PASSES_2)
+            mark_used("ybr", unit)
+            part, q = unit // LINE_BLOCKS, unit % LINE_BLOCKS
+            for g in range(PASSES_2):
+                waiting.append((grouped[:, g, :], ybr_codes[:, g, q, part, :], ybr_scales[:, g, q, part, :]))
 
         for t in range(IM_TILES):
             im_codes = im_pool.tile([P, PASSES_1, P], U32, align_bytes=64)
@@ -226,7 +221,7 @@ def tile_pinnlayer_pa_k_kernel(tc, Volt, IM, Ybr, n_o_mu_i_u, out):
                 quantise_waiting()
                 sort_next()
                 grouped = transpose_banks(
-                    in_order[("im", chunk)][:].rearrange("p (b s) h w -> p b s h w", s=2), IM_CHUNK_PASSES // 2, "chunk"
+                    in_order[("im", chunk)][:].rearrange("p (b s) h w -> p b s h w", s=2), IM_CHUNK_PASSES // 2
                 )
                 passes = slice(c * IM_CHUNK_PASSES, (c + 1) * IM_CHUNK_PASSES)
                 waiting.append(
@@ -238,22 +233,10 @@ def tile_pinnlayer_pa_k_kernel(tc, Volt, IM, Ybr, n_o_mu_i_u, out):
                 )
                 if c == 0 and t >= 3 and t % 2 == 1:
                     round_dv((t - 3) // 2)
-            if t >= FIRST_YBR_STEP:
-                ybr_banks((t - FIRST_YBR_STEP) * YBR_BANKS_A_STEP, YBR_BANKS_A_STEP)
-            if t == FIRST_YBR_STEP:
+            if 0 <= t - FIRST_YBR_STEP < YBR_UNITS:
+                transpose_ybr(t - FIRST_YBR_STEP)
+            if t == IM_TILES - 2:
                 nc.sync.dma_start(out=mu[:], in_=n_o_mu_i_u.rearrange("(t p) l -> p t l", p=P))
-            if t == FIRST_YBR_STEP + 2:
-                for s in range(SAMPLE_TILES):
-                    negative_part = work.tile([P, LINES], F32)
-                    nc.scalar.activation(
-                        out=negative_part[:], in_=mu[:, s, :], func=ACT.Relu, scale=-2.0,
-                        accum_out=terms[:, s, 0, LINE_BLOCKS : LINE_BLOCKS + 1],
-                    )
-                    nc.scalar.activation(out=mu_size[:, s, :], in_=mu[:, s, :], func=ACT.Abs)
-                    nc.gpsimd.tensor_scalar(
-                        out=weight[:, s, :], in0=mu_size[:, s, :], scalar1=2.0, scalar2=1.0,
-                        op0=ALU.mult, op1=ALU.add,
-                    )
             if t >= 1:
                 first_matmul(t - 1, range(PASSES_1))
 
@@ -262,6 +245,8 @@ def tile_pinnlayer_pa_k_kernel(tc, Volt, IM, Ybr, n_o_mu_i_u, out):
 
         def second_matmul(q, t, passes):
             samples = slice(t * P, (t + 1) * P)
+            if (q, t) not in ibr:
+                ibr[(q, t)] = bank_pool.tile([P, 2 * BANK_COLS], F32, tag="bank", name="ibr")
             for g in passes:
                 nc.tensor.matmul_mx(
                     out=ibr[(q, t)][:],
@@ -275,10 +260,20 @@ def tile_pinnlayer_pa_k_kernel(tc, Volt, IM, Ybr, n_o_mu_i_u, out):
 
         blocks = [(q, t) for q in range(LINE_BLOCKS) for t in range(SAMPLE_TILES)]
         first_matmul(IM_TILES - 1, range(PASSES_1))
-        for q, t in blocks:
-            ibr[(q, t)] = bank_pool.tile([P, 2 * BANK_COLS], F32, tag="bank", name="ibr")
+        for q, t in blocks[:EARLY_BLOCKS]:
             second_matmul(q, t, range(PASSES_2 - 1))
         round_dv(IM_TILES // 2 - 1)
+        for s in range(SAMPLE_TILES):
+            negative_part = work.tile([P, LINES], F32)
+            nc.scalar.activation(
+                out=negative_part[:], in_=mu[:, s, :], func=ACT.Relu, scale=-2.0,
+                accum_out=terms[:, s, 0, LINE_BLOCKS : LINE_BLOCKS + 1],
+            )
+            mu_size = work.tile([P, LINES], F32)
+            nc.scalar.activation(out=mu_size[:], in_=mu[:, s, :], func=ACT.Abs)
+            nc.vector.tensor_scalar(
+                out=weight[:, s, :], in0=mu_size[:], scalar1=2.0, scalar2=1.0, op0=ALU.mult, op1=ALU.add
+            )
 
         def weighted_sum(q, t, i_up):
             i_size = work.tile([P, BANK_COLS], F32)
@@ -291,7 +286,7 @@ def tile_pinnlayer_pa_k_kernel(tc, Volt, IM, Ybr, n_o_mu_i_u, out):
 
         block_before = None
         for q, t in blocks:
-            second_matmul(q, t, range(PASSES_2 - 1, PASSES_2))
+            second_matmul(q, t, range(PASSES_2 - 1 if (q, t) in ibr else 0, PASSES_2))
             squares = work.tile([P, 2, BANK_COLS], F32)
             nc.scalar.activation(
                 out=squares[:].rearrange("p c n -> p (c n)"), in_=ibr[(q, t)][:], func=ACT.Square,

@@ -14,7 +14,6 @@ ACT = mybir.ActivationFunctionType
 P = 128
 PACK = 4
 K_PASS = P * PACK
-RUN = 8
 
 SAMPLES = 256
 VOLTS = 8192
@@ -38,7 +37,8 @@ FIRST_YBR_STEP = IM_TILES - YBR_UNITS
 LINE_BLOCKS = LINES // BANK_COLS
 
 RAW_TILES = 7
-SORT_AHEAD = 2
+SORT_AHEAD = 3
+SORTED_BANKS = 4
 
 EARLY_BLOCKS = 3
 
@@ -84,13 +84,17 @@ def tile_pinnlayer_pa_k_kernel(tc, Volt, IM, Ybr, n_o_mu_i_u, out):
         volt_chunk_k = VOLT_CHUNK_PASSES * K_PASS
         im_chunk_k = IM_CHUNK_PASSES * K_PASS
 
-        load_order = [("volt", c) for c in range(VOLT_CHUNKS)]
+        load_order = [("volt", n) for n in range(VOLT_CHUNKS)]
         for t in range(IM_TILES):
-            load_order.extend([("im", t * IM_CHUNKS + c) for c in range(IM_CHUNKS)])
+            chunks = [("im", t * IM_CHUNKS + c) for c in range(IM_CHUNKS)]
+            load_order.extend(chunks)
             if 0 <= t - FIRST_YBR_STEP < YBR_UNITS:
                 load_order.append(("ybr", t - FIRST_YBR_STEP))
         used = {}
         raw = {}
+
+        def value_of_tile(t):
+            return 2 * (t % 2) + t % PACK // 2
 
         def load(kind, n):
             if kind == "volt":
@@ -99,7 +103,7 @@ def tile_pinnlayer_pa_k_kernel(tc, Volt, IM, Ybr, n_o_mu_i_u, out):
             elif kind == "im":
                 tile = raw_pool.tile([P, im_chunk_k], BF16, tag="raw")
                 t, c = n // IM_CHUNKS, n % IM_CHUNKS
-                source = im_rows[t // PACK, t % PACK, :, c * im_chunk_k : (c + 1) * im_chunk_k]
+                source = im_rows[t // PACK, value_of_tile(t), :, c * im_chunk_k : (c + 1) * im_chunk_k]
             else:
                 tile = raw_pool.tile([P, 2, CURRENTS], BF16, tag="raw")
                 source = ybr_rows[n]
@@ -111,28 +115,28 @@ def tile_pinnlayer_pa_k_kernel(tc, Volt, IM, Ybr, n_o_mu_i_u, out):
             while len(raw) < len(load_order) and load_order[len(raw) - RAW_TILES] in used:
                 load(*load_order[len(raw)])
 
-        def sort_words(kind, n, sets):
-            tile = raw[(kind, n)]
-            tile_in_order = sorted_pool.tile([P, sets, 2, P], F32, tag="sorted")
-            flat = tile[:].rearrange("p s k -> p (s k)") if kind == "volt" else tile[:]
+        def sort_words(chunk):
+            passes = 2 * SORTED_BANKS
+            tile = sorted_pool.tile([P, passes, 2, P], F32, tag="sorted", name="sorted_words")
             nc.vector.tensor_copy(
-                out=tile_in_order[:].rearrange("p a h (m j) -> p a h m j", j=RUN),
-                in_=flat.bitcast(F32).rearrange("p (a m h j) -> p a h m j", a=sets, h=2, j=RUN),
+                out=tile[:],
+                in_=raw[("im", chunk)][:, : passes * K_PASS].bitcast(F32).rearrange("p (a w h) -> p a h w", a=passes, h=2),
             )
-            mark_used(kind, n)
-            return tile_in_order
+            return tile
 
-        def transpose_banks(words, n_banks):
-            grouped = grouped_pool.tile([P, n_banks, 2 * P * PACK], BF16, tag="grouped", align_bytes=64)
-            for bank in range(n_banks):
+        def transpose_banks(words, vector_banks=()):
+            grouped = grouped_pool.tile([P, len(words), 2 * P * PACK], BF16, tag="grouped", align_bytes=64)
+            for bank in range(len(words)):
                 flipped = bank_pool.tile([P, 2, 2, P], F32, tag="bank")
                 for s in range(2):
                     for h in range(2):
-                        nc.tensor.transpose(flipped[:, s, h, :], words[:, bank, s, h, :], identity[:])
-                nc.scalar.copy(
-                    out=grouped[:, bank, :].bitcast(F32).rearrange("p (s r h) -> p s r h", s=2, h=2),
-                    in_=flipped[:].rearrange("p s h r -> p s r h"),
-                )
+                        nc.tensor.transpose(flipped[:, s, h, :], words[bank][:, s, h, :], identity[:])
+                pairs_out = grouped[:, bank, :].bitcast(F32).rearrange("p (s r h) -> p s r h", s=2, h=2)
+                pairs_in = flipped[:].rearrange("p s h r -> p s r h")
+                if bank in vector_banks:
+                    nc.vector.tensor_copy(out=pairs_out, in_=pairs_in)
+                else:
+                    nc.scalar.copy(out=pairs_out, in_=pairs_in)
             return grouped
 
         def quantise(grouped, codes, scales):
@@ -148,25 +152,21 @@ def tile_pinnlayer_pa_k_kernel(tc, Volt, IM, Ybr, n_o_mu_i_u, out):
                 quantise(*operands)
             waiting.clear()
 
-        sort_order = [("volt", c, SAMPLE_TILES * VOLT_CHUNK_PASSES) for c in range(VOLT_CHUNKS)]
-        sort_order.extend([("im", chunk, IM_CHUNK_PASSES) for chunk in range(IM_TILES * IM_CHUNKS)])
         in_order = {}
 
-        def sort_next():
-            if sort_order:
-                kind, n, sets = sort_order[0]
-                sort_order.remove(sort_order[0])
-                in_order[(kind, n)] = sort_words(kind, n, sets)
+        def sort_up_to(kind, n):
+            for kind_after, chunk in load_order[: load_order.index((kind, n)) + SORT_AHEAD + 1]:
+                if kind_after == "im" and chunk not in in_order:
+                    in_order[chunk] = sort_words(chunk)
+                    if SORTED_BANKS == 4:
+                        mark_used(kind_after, chunk)
 
-        for chunk in range(SORT_AHEAD):
-            sort_next()
-
-        for c in range(VOLT_CHUNKS):
-            sort_next()
-            grouped = transpose_banks(
-                in_order[("volt", c)][:].rearrange("p (s b) h w -> p b s h w", s=SAMPLE_TILES), VOLT_CHUNK_PASSES
-            )
+        def transpose_volt(c):
+            words = raw[("volt", c)][:].bitcast(F32).rearrange("p s (b w h) -> p b s h w", b=VOLT_CHUNK_PASSES, h=2)
             quantise_waiting()
+            sort_up_to("volt", c)
+            grouped = transpose_banks([words[:, b] for b in range(VOLT_CHUNK_PASSES)])
+            mark_used("volt", c)
             passes = slice(c * VOLT_CHUNK_PASSES, (c + 1) * VOLT_CHUNK_PASSES)
             waiting.append(
                 (
@@ -176,17 +176,51 @@ def tile_pinnlayer_pa_k_kernel(tc, Volt, IM, Ybr, n_o_mu_i_u, out):
                 )
             )
 
-        acc_tiles = {}
         im_tiles = {}
 
-        def first_matmul(t, passes):
+        def transpose_im(t, c):
+            if t not in im_tiles:
+                im_codes = im_pool.tile([P, PASSES_1, P], U32, align_bytes=64)
+                im_scales = im_pool.tile([P, PASSES_1, P], U8, align_bytes=64)
+                im_tiles[t] = (im_codes, im_scales)
             im_codes, im_scales = im_tiles[t]
-            pair, e = t // 2, t % 2
-            if pair not in acc_tiles:
-                acc_tiles[pair] = acc_pool.tile([P, 2, SAMPLES], F32, tag="acc", name="acc")
-            for a in passes:
+            chunk = t * IM_CHUNKS + c
+            quantise_waiting()
+            sort_up_to("im", chunk)
+            words = in_order[chunk][:].rearrange("p (b s) h w -> p b s h w", s=2)
+            views = [words[:, b] for b in range(SORTED_BANKS)]
+            words = raw[("im", chunk)][:].bitcast(F32).rearrange("p (b s w h) -> p b s h w", s=2, w=P, h=2)
+            views.extend([words[:, b] for b in range(SORTED_BANKS, IM_CHUNK_PASSES // 2)])
+            grouped = transpose_banks(views)
+            if SORTED_BANKS < 4:
+                mark_used("im", chunk)
+            passes = slice(c * IM_CHUNK_PASSES, (c + 1) * IM_CHUNK_PASSES)
+            waiting.append(
+                (
+                    grouped[:].rearrange("p b v -> p (b v)"),
+                    im_codes[:, passes, :].rearrange("p a r -> p (a r)"),
+                    im_scales[:, passes, :].rearrange("p a r -> p (a r)"),
+                )
+            )
+
+        def transpose_ybr(unit):
+            words = raw[("ybr", unit)][:].bitcast(F32).rearrange("p s (g w h) -> p g s h w", g=PASSES_2, h=2)
+            grouped = transpose_banks([words[:, g] for g in range(PASSES_2)])
+            mark_used("ybr", unit)
+            part, q = unit // LINE_BLOCKS, unit % LINE_BLOCKS
+            for g in range(PASSES_2):
+                waiting.append((grouped[:, g, :], ybr_codes[:, g, q, part, :], ybr_scales[:, g, q, part, :]))
+
+        dv_banks = {}
+
+        def first_matmul(t, chunks):
+            im_codes, im_scales = im_tiles[t]
+            bank = (t // PACK, t % 2)
+            if bank not in dv_banks:
+                dv_banks[bank] = acc_pool.tile([P, 2, SAMPLES], F32, tag="acc", name="acc")
+            for a in range(chunks[0] * IM_CHUNK_PASSES, (chunks[-1] + 1) * IM_CHUNK_PASSES):
                 nc.tensor.matmul_mx(
-                    out=acc_tiles[pair][:, e, :],
+                    out=dv_banks[bank][:, t % PACK // 2, :],
                     lhsT=im_codes[:, a, :].bitcast(FP8X4),
                     lhsT_scale=im_scales[:, a, :],
                     rhs=volt_codes[:, a, :].bitcast(FP8X4),
@@ -195,52 +229,32 @@ def tile_pinnlayer_pa_k_kernel(tc, Volt, IM, Ybr, n_o_mu_i_u, out):
                     stop=(a == PASSES_1 - 1),
                 )
 
-        def round_dv(pair):
-            g, u = pair // 2, pair % 2
+        def round_dv(g, b):
             nc.vector.tensor_copy(
-                out=dv_grouped[:, g, :, 2 * u : 2 * u + 2],
-                in_=acc_tiles[pair][:].rearrange("p e b -> p b e"),
+                out=dv_grouped[:, g, :, 2 * b : 2 * b + 2], in_=dv_banks[(g, b)][:].rearrange("p e n -> p n e")
             )
-            if u == 1:
-                quantise(dv_grouped[:, g].rearrange("p b t -> p (b t)"), dv_codes[:, g, :], dv_scales[:, g, :])
+            if b == 1:
+                quantise(dv_grouped[:, g].rearrange("p n v -> p (n v)"), dv_codes[:, g, :], dv_scales[:, g, :])
 
-        def transpose_ybr(unit):
-            words = raw[("ybr", unit)][:].bitcast(F32).rearrange("p s (g w h) -> p g s h w", g=PASSES_2, h=2)
-            grouped = transpose_banks(words, PASSES_2)
-            mark_used("ybr", unit)
-            part, q = unit // LINE_BLOCKS, unit % LINE_BLOCKS
-            for g in range(PASSES_2):
-                waiting.append((grouped[:, g, :], ybr_codes[:, g, q, part, :], ybr_scales[:, g, q, part, :]))
+        for c in range(VOLT_CHUNKS):
+            transpose_volt(c)
 
         for t in range(IM_TILES):
-            im_codes = im_pool.tile([P, PASSES_1, P], U32, align_bytes=64)
-            im_scales = im_pool.tile([P, PASSES_1, P], U8, align_bytes=64)
-            im_tiles[t] = (im_codes, im_scales)
-            for c in range(IM_CHUNKS):
-                chunk = t * IM_CHUNKS + c
-                quantise_waiting()
-                sort_next()
-                grouped = transpose_banks(
-                    in_order[("im", chunk)][:].rearrange("p (b s) h w -> p b s h w", s=2), IM_CHUNK_PASSES // 2
-                )
-                passes = slice(c * IM_CHUNK_PASSES, (c + 1) * IM_CHUNK_PASSES)
-                waiting.append(
-                    (
-                        grouped[:].rearrange("p b v -> p (b v)"),
-                        im_codes[:, passes, :].rearrange("p a r -> p (a r)"),
-                        im_scales[:, passes, :].rearrange("p a r -> p (a r)"),
-                    )
-                )
-                if c == 0 and t >= 3 and t % 2 == 1:
-                    round_dv((t - 3) // 2)
+            transpose_im(t, 0)
+            if t >= 4:
+                done = t - 2
+                if done % PACK >= 2:
+                    round_dv(done // PACK, done % 2)
+            transpose_im(t, 1)
             if 0 <= t - FIRST_YBR_STEP < YBR_UNITS:
                 transpose_ybr(t - FIRST_YBR_STEP)
             if t == IM_TILES - 2:
                 nc.sync.dma_start(out=mu[:], in_=n_o_mu_i_u.rearrange("(t p) l -> p t l", p=P))
             if t >= 1:
-                first_matmul(t - 1, range(PASSES_1))
+                first_matmul(t - 1, [0, 1])
 
         quantise_waiting()
+        round_dv(PASSES_2 - 1, 0)
         ibr = {}
 
         def second_matmul(q, t, passes):
@@ -259,10 +273,10 @@ def tile_pinnlayer_pa_k_kernel(tc, Volt, IM, Ybr, n_o_mu_i_u, out):
                 )
 
         blocks = [(q, t) for q in range(LINE_BLOCKS) for t in range(SAMPLE_TILES)]
-        first_matmul(IM_TILES - 1, range(PASSES_1))
+        first_matmul(IM_TILES - 1, [0, 1])
         for q, t in blocks[:EARLY_BLOCKS]:
             second_matmul(q, t, range(PASSES_2 - 1))
-        round_dv(IM_TILES // 2 - 1)
+        round_dv(PASSES_2 - 1, 1)
         for s in range(SAMPLE_TILES):
             negative_part = work.tile([P, LINES], F32)
             nc.scalar.activation(

@@ -245,13 +245,15 @@ def tile_pinnlayer_pa_k_kernel(tc, Volt, IM, Ybr, n_o_mu_i_u, out):
                 done = t - 2
                 if done % PACK >= 2:
                     round_dv(done // PACK, done % 2)
+            if t >= 1:
+                first_matmul(t - 1, [0])
             transpose_im(t, 1)
             if 0 <= t - FIRST_YBR_STEP < YBR_UNITS:
                 transpose_ybr(t - FIRST_YBR_STEP)
             if t == IM_TILES - 2:
                 nc.sync.dma_start(out=mu[:], in_=n_o_mu_i_u.rearrange("(t p) l -> p t l", p=P))
             if t >= 1:
-                first_matmul(t - 1, [0, 1])
+                first_matmul(t - 1, [1])
 
         quantise_waiting()
         round_dv(PASSES_2 - 1, 0)

@@ -27,18 +27,16 @@ SAMPLE_TILES = SAMPLES // P
 
 BANK_COLS = 2 * P
 
-VOLT_CHUNK_PASSES = 2
+VOLT_CHUNK_PASSES = 4
 VOLT_CHUNKS = PASSES_1 // VOLT_CHUNK_PASSES
 IM_CHUNK_PASSES = 8
 IM_TILES = CURRENTS // P
 IM_CHUNKS = PASSES_1 // IM_CHUNK_PASSES
 YBR_UNITS = CURRENTS // BANK_COLS
-FIRST_YBR_STEP = IM_TILES - YBR_UNITS
 LINE_BLOCKS = LINES // BANK_COLS
 
 RAW_TILES = 7
-SORT_AHEAD = 3
-SORTED_BANKS = 4
+FIRST_YBR_TILE = IM_TILES - YBR_UNITS
 
 EARLY_BLOCKS = 3
 
@@ -50,10 +48,11 @@ def tile_pinnlayer_pa_k_kernel(tc, Volt, IM, Ybr, n_o_mu_i_u, out):
     with ExitStack() as ctx:
         keep = ctx.enter_context(tc.tile_pool(name="keep", bufs=1))
         raw_pool = ctx.enter_context(tc.tile_pool(name="raw", bufs=RAW_TILES))
-        sorted_pool = ctx.enter_context(tc.tile_pool(name="sorted", bufs=SORT_AHEAD + 2))
+        sorted_pool = ctx.enter_context(tc.tile_pool(name="sorted", bufs=3))
         grouped_pool = ctx.enter_context(tc.tile_pool(name="grouped", bufs=3))
         im_pool = ctx.enter_context(tc.tile_pool(name="im", bufs=2))
         work = ctx.enter_context(tc.tile_pool(name="work", bufs=2))
+        sums = ctx.enter_context(tc.tile_pool(name="sums", bufs=4))
         bank_pool = ctx.enter_context(tc.psum_pool(name="bank", bufs=6))
         acc_pool = ctx.enter_context(tc.psum_pool(name="acc", bufs=2))
         ctx.enter_context(tc.manual_schedule())
@@ -80,16 +79,15 @@ def tile_pinnlayer_pa_k_kernel(tc, Volt, IM, Ybr, n_o_mu_i_u, out):
 
         volt_rows = Volt.rearrange("(s p) k -> p s k", p=P)
         im_rows = IM.rearrange("(g p t) k -> g t p k", g=PASSES_2, p=P, t=PACK)
-        ybr_rows = Ybr.rearrange("(n s p) l -> n p s l", n=YBR_UNITS, s=2, p=P)
+        ybr_rows = Ybr.rearrange("(n p s) l -> n p (s l)", n=YBR_UNITS, s=2, p=P)
         volt_chunk_k = VOLT_CHUNK_PASSES * K_PASS
         im_chunk_k = IM_CHUNK_PASSES * K_PASS
 
         load_order = [("volt", n) for n in range(VOLT_CHUNKS)]
         for t in range(IM_TILES):
-            chunks = [("im", t * IM_CHUNKS + c) for c in range(IM_CHUNKS)]
-            load_order.extend(chunks)
-            if 0 <= t - FIRST_YBR_STEP < YBR_UNITS:
-                load_order.append(("ybr", t - FIRST_YBR_STEP))
+            load_order.extend([("im", t * IM_CHUNKS + c) for c in range(IM_CHUNKS)])
+            if t >= FIRST_YBR_TILE:
+                load_order.append(("ybr", t - FIRST_YBR_TILE))
         used = {}
         raw = {}
 
@@ -105,7 +103,7 @@ def tile_pinnlayer_pa_k_kernel(tc, Volt, IM, Ybr, n_o_mu_i_u, out):
                 t, c = n // IM_CHUNKS, n % IM_CHUNKS
                 source = im_rows[t // PACK, value_of_tile(t), :, c * im_chunk_k : (c + 1) * im_chunk_k]
             else:
-                tile = raw_pool.tile([P, 2, CURRENTS], BF16, tag="raw")
+                tile = raw_pool.tile([P, 2 * CURRENTS], BF16, tag="raw")
                 source = ybr_rows[n]
             nc.sync.dma_start(out=tile[:], in_=source)
             raw[(kind, n)] = tile
@@ -116,15 +114,15 @@ def tile_pinnlayer_pa_k_kernel(tc, Volt, IM, Ybr, n_o_mu_i_u, out):
                 load(*load_order[len(raw)])
 
         def sort_words(chunk):
-            passes = 2 * SORTED_BANKS
+            passes = IM_CHUNK_PASSES
             tile = sorted_pool.tile([P, passes, 2, P], F32, tag="sorted", name="sorted_words")
             nc.vector.tensor_copy(
                 out=tile[:],
-                in_=raw[("im", chunk)][:, : passes * K_PASS].bitcast(F32).rearrange("p (a w h) -> p a h w", a=passes, h=2),
+                in_=raw[("im", chunk)][:].bitcast(F32).rearrange("p (a w h) -> p a h w", a=passes, h=2),
             )
             return tile
 
-        def transpose_banks(words, vector_banks=()):
+        def transpose_banks(words):
             grouped = grouped_pool.tile([P, len(words), 2 * P * PACK], BF16, tag="grouped", align_bytes=64)
             for bank in range(len(words)):
                 flipped = bank_pool.tile([P, 2, 2, P], F32, tag="bank")
@@ -133,10 +131,7 @@ def tile_pinnlayer_pa_k_kernel(tc, Volt, IM, Ybr, n_o_mu_i_u, out):
                         nc.tensor.transpose(flipped[:, s, h, :], words[bank][:, s, h, :], identity[:])
                 pairs_out = grouped[:, bank, :].bitcast(F32).rearrange("p (s r h) -> p s r h", s=2, h=2)
                 pairs_in = flipped[:].rearrange("p s h r -> p s r h")
-                if bank in vector_banks:
-                    nc.vector.tensor_copy(out=pairs_out, in_=pairs_in)
-                else:
-                    nc.scalar.copy(out=pairs_out, in_=pairs_in)
+                nc.scalar.copy(out=pairs_out, in_=pairs_in)
             return grouped
 
         def quantise(grouped, codes, scales):
@@ -154,17 +149,16 @@ def tile_pinnlayer_pa_k_kernel(tc, Volt, IM, Ybr, n_o_mu_i_u, out):
 
         in_order = {}
 
-        def sort_up_to(kind, n):
-            for kind_after, chunk in load_order[: load_order.index((kind, n)) + SORT_AHEAD + 1]:
-                if kind_after == "im" and chunk not in in_order:
+        def sort_up_to(last):
+            for chunk in range(min(last + 1, IM_TILES * IM_CHUNKS)):
+                if chunk not in in_order:
                     in_order[chunk] = sort_words(chunk)
-                    if SORTED_BANKS == 4:
-                        mark_used(kind_after, chunk)
+                    mark_used("im", chunk)
 
         def transpose_volt(c):
             words = raw[("volt", c)][:].bitcast(F32).rearrange("p s (b w h) -> p b s h w", b=VOLT_CHUNK_PASSES, h=2)
             quantise_waiting()
-            sort_up_to("volt", c)
+            sort_up_to(c - VOLT_CHUNKS + 1)
             grouped = transpose_banks([words[:, b] for b in range(VOLT_CHUNK_PASSES)])
             mark_used("volt", c)
             passes = slice(c * VOLT_CHUNK_PASSES, (c + 1) * VOLT_CHUNK_PASSES)
@@ -185,15 +179,10 @@ def tile_pinnlayer_pa_k_kernel(tc, Volt, IM, Ybr, n_o_mu_i_u, out):
                 im_tiles[t] = (im_codes, im_scales)
             im_codes, im_scales = im_tiles[t]
             chunk = t * IM_CHUNKS + c
+            sort_up_to(chunk + 1)
             quantise_waiting()
-            sort_up_to("im", chunk)
             words = in_order[chunk][:].rearrange("p (b s) h w -> p b s h w", s=2)
-            views = [words[:, b] for b in range(SORTED_BANKS)]
-            words = raw[("im", chunk)][:].bitcast(F32).rearrange("p (b s w h) -> p b s h w", s=2, w=P, h=2)
-            views.extend([words[:, b] for b in range(SORTED_BANKS, IM_CHUNK_PASSES // 2)])
-            grouped = transpose_banks(views)
-            if SORTED_BANKS < 4:
-                mark_used("im", chunk)
+            grouped = transpose_banks([words[:, b] for b in range(IM_CHUNK_PASSES // 2)])
             passes = slice(c * IM_CHUNK_PASSES, (c + 1) * IM_CHUNK_PASSES)
             waiting.append(
                 (
@@ -204,7 +193,7 @@ def tile_pinnlayer_pa_k_kernel(tc, Volt, IM, Ybr, n_o_mu_i_u, out):
             )
 
         def transpose_ybr(unit):
-            words = raw[("ybr", unit)][:].bitcast(F32).rearrange("p s (g w h) -> p g s h w", g=PASSES_2, h=2)
+            words = raw[("ybr", unit)][:].bitcast(F32).rearrange("p (s g w h) -> p g s h w", s=2, g=PASSES_2, h=2)
             grouped = transpose_banks([words[:, g] for g in range(PASSES_2)])
             mark_used("ybr", unit)
             part, q = unit // LINE_BLOCKS, unit % LINE_BLOCKS
@@ -239,24 +228,34 @@ def tile_pinnlayer_pa_k_kernel(tc, Volt, IM, Ybr, n_o_mu_i_u, out):
         for c in range(VOLT_CHUNKS):
             transpose_volt(c)
 
-        for t in range(IM_TILES):
-            transpose_im(t, 0)
-            if t >= 4:
-                done = t - 2
-                if done % PACK >= 2:
-                    round_dv(done // PACK, done % 2)
-            if t >= 1:
-                first_matmul(t - 1, [0])
-            transpose_im(t, 1)
-            if 0 <= t - FIRST_YBR_STEP < YBR_UNITS:
-                transpose_ybr(t - FIRST_YBR_STEP)
-            if t == IM_TILES - 2:
-                nc.sync.dma_start(out=mu[:], in_=n_o_mu_i_u.rearrange("(t p) l -> p t l", p=P))
-            if t >= 1:
-                first_matmul(t - 1, [1])
+        complete = []
 
+        multiplied = []
+
+        def multiply(last):
+            for chunk in range(len(multiplied), last + 1):
+                t, c = chunk // IM_CHUNKS, chunk % IM_CHUNKS
+                first_matmul(t, [c])
+                multiplied.append(chunk)
+                if c == IM_CHUNKS - 1 and t % PACK >= 2:
+                    complete.append((t // PACK, t % 2))
+
+        for chunk in range(IM_TILES * IM_CHUNKS):
+            t, c = chunk // IM_CHUNKS, chunk % IM_CHUNKS
+            transpose_im(t, c)
+            if complete:
+                round_dv(*complete[0])
+                complete.clear()
+            if c == IM_CHUNKS - 1 and t >= FIRST_YBR_TILE:
+                transpose_ybr(t - FIRST_YBR_TILE)
+            if c == 0 and t == IM_TILES - 2:
+                nc.sync.dma_start(out=mu[:], in_=n_o_mu_i_u.rearrange("(t p) l -> p t l", p=P))
+            multiply(chunk - 2)
+        multiply(IM_TILES * IM_CHUNKS - 2)
         quantise_waiting()
+        multiply(IM_TILES * IM_CHUNKS - 1)
         round_dv(PASSES_2 - 1, 0)
+
         ibr = {}
 
         def second_matmul(q, t, passes):
@@ -275,7 +274,6 @@ def tile_pinnlayer_pa_k_kernel(tc, Volt, IM, Ybr, n_o_mu_i_u, out):
                 )
 
         blocks = [(q, t) for q in range(LINE_BLOCKS) for t in range(SAMPLE_TILES)]
-        first_matmul(IM_TILES - 1, [0, 1])
         for q, t in blocks[:EARLY_BLOCKS]:
             second_matmul(q, t, range(PASSES_2 - 1))
         round_dv(PASSES_2 - 1, 1)
@@ -292,31 +290,36 @@ def tile_pinnlayer_pa_k_kernel(tc, Volt, IM, Ybr, n_o_mu_i_u, out):
             )
 
         def weighted_sum(q, t, i_up):
-            i_size = work.tile([P, BANK_COLS], F32)
+            i_size = sums.tile([P, BANK_COLS], F32)
             nc.scalar.activation(out=i_size[:], in_=i_up[:], func=ACT.Abs)
-            weighted = work.tile([P, BANK_COLS], F32)
+            weighted = sums.tile([P, BANK_COLS], F32)
             nc.vector.scalar_tensor_tensor(
-                out=weighted[:], in0=i_size[:], scalar=1.0, in1=weight[:, t, q * BANK_COLS : (q + 1) * BANK_COLS],
+                out=weighted[:].rearrange("p (s r) -> p s r", s=2),
+                in0=i_size[:].rearrange("p (s r) -> p s r", s=2),
+                scalar=1.0,
+                in1=weight[:, t, q * BANK_COLS : (q + 1) * BANK_COLS].rearrange("p (r s) -> p s r", s=2),
                 op0=ALU.mult, op1=ALU.mult, accum_out=terms[:, t, 1, q : q + 1],
             )
 
-        block_before = None
+        not_summed = []
         for q, t in blocks:
             second_matmul(q, t, range(PASSES_2 - 1 if (q, t) in ibr else 0, PASSES_2))
-            squares = work.tile([P, 2, BANK_COLS], F32)
+            squares = sums.tile([P, 2, BANK_COLS], F32)
             nc.scalar.activation(
                 out=squares[:].rearrange("p c n -> p (c n)"), in_=ibr[(q, t)][:], func=ACT.Square,
                 accum_out=terms[:, t, 0, q : q + 1],
             )
-            i_up = work.tile([P, BANK_COLS], F32)
+            i_up = sums.tile([P, BANK_COLS], F32)
             nc.vector.scalar_tensor_tensor(
                 out=i_up[:], in0=squares[:, 0, :], scalar=-LIMIT_SQUARED, in1=squares[:, 1, :],
                 op0=ALU.add, op1=ALU.add,
             )
-            if block_before is not None:
-                weighted_sum(*block_before)
-            block_before = (q, t, i_up)
-        weighted_sum(*block_before)
+            not_summed.append((q, t, i_up))
+            if len(not_summed) > 3:
+                weighted_sum(*not_summed[0])
+                not_summed.remove(not_summed[0])
+        for block in not_summed:
+            weighted_sum(*block)
 
         nc.vector.tensor_reduce(
             out=totals[:, 0:SAMPLE_TILES], in_=terms[:].rearrange("p t w c -> p t (w c)"),

from contextlib import ExitStack

import concourse.mybir as mybir
from concourse.masks import make_identity

F32 = mybir.dt.float32
BF16 = mybir.dt.bfloat16
U32 = mybir.dt.uint32
U8 = mybir.dt.uint8
FP8X4 = mybir.dt.float8_e4m3fn_x4
ALU = mybir.AluOpType
ACT = mybir.ActivationFunctionType

P = 128
PACK = 4
K_PASS = P * PACK

SAMPLES = 256
VOLTS = 8192
CURRENTS = 1536
LINES = CURRENTS // 2
LIMIT_SQUARED = 1.0

PASSES_1 = VOLTS // K_PASS
PASSES_2 = CURRENTS // K_PASS
SAMPLE_TILES = SAMPLES // P

BANK_COLS = 2 * P

VOLT_CHUNK_PASSES = 4
VOLT_CHUNKS = PASSES_1 // VOLT_CHUNK_PASSES
IM_CHUNK_PASSES = 8
IM_TILES = CURRENTS // P
IM_CHUNKS = PASSES_1 // IM_CHUNK_PASSES
YBR_UNITS = CURRENTS // BANK_COLS
LINE_BLOCKS = LINES // BANK_COLS

RAW_TILES = 7
FIRST_YBR_TILE = IM_TILES - YBR_UNITS

EARLY_BLOCKS = 3

FLOPS = 2 * SAMPLES * CURRENTS * (VOLTS + CURRENTS)


def tile_pinnlayer_pa_k_kernel(tc, Volt, IM, Ybr, n_o_mu_i_u, out):
    nc = tc.nc
    with ExitStack() as ctx:
        keep = ctx.enter_context(tc.tile_pool(name="keep", bufs=1))
        raw_pool = ctx.enter_context(tc.tile_pool(name="raw", bufs=RAW_TILES))
        sorted_pool = ctx.enter_context(tc.tile_pool(name="sorted", bufs=3))
        grouped_pool = ctx.enter_context(tc.tile_pool(name="grouped", bufs=3))
        im_pool = ctx.enter_context(tc.tile_pool(name="im", bufs=2))
        work = ctx.enter_context(tc.tile_pool(name="work", bufs=2))
        sums = ctx.enter_context(tc.tile_pool(name="sums", bufs=4))
        bank_pool = ctx.enter_context(tc.psum_pool(name="bank", bufs=6))
        acc_pool = ctx.enter_context(tc.psum_pool(name="acc", bufs=2))
        ctx.enter_context(tc.manual_schedule())

        identity = keep.tile([P, P], F32)
        make_identity(nc, identity[:])

        terms = keep.tile([P, SAMPLE_TILES, 2, 8], F32)
        nc.vector.memset(terms[:], 0.0)
        totals = keep.tile([P, P], F32)
        nc.vector.memset(totals[:], 0.0)
        table_warmer = keep.tile([P, 1], F32)
        nc.scalar.activation(out=table_warmer[:], in_=totals[:, 0:1], func=ACT.Abs)

        volt_codes = keep.tile([P, PASSES_1, SAMPLES], U32, align_bytes=64)
        volt_scales = keep.tile([P, PASSES_1, SAMPLES], U8, align_bytes=64)
        ybr_codes = keep.tile([P, PASSES_2, LINE_BLOCKS, 2, BANK_COLS], U32, align_bytes=64)
        ybr_scales = keep.tile([P, PASSES_2, LINE_BLOCKS, 2, BANK_COLS], U8, align_bytes=64)
        dv_grouped = keep.tile([P, PASSES_2, SAMPLES, PACK], BF16, align_bytes=64)
        dv_codes = keep.tile([P, PASSES_2, SAMPLES], U32, align_bytes=64)
        dv_scales = keep.tile([P, PASSES_2, SAMPLES], U8, align_bytes=64)
        mu = keep.tile([P, SAMPLE_TILES, LINES], BF16)
        weight = keep.tile([P, SAMPLE_TILES, LINES], F32)

        volt_rows = Volt.rearrange("(s p) k -> p s k", p=P)
        im_rows = IM.rearrange("(g p t) k -> g t p k", g=PASSES_2, p=P, t=PACK)
        ybr_rows = Ybr.rearrange("(n p s) l -> n p (s l)", n=YBR_UNITS, s=2, p=P)
        volt_chunk_k = VOLT_CHUNK_PASSES * K_PASS
        im_chunk_k = IM_CHUNK_PASSES * K_PASS

        load_order = [("volt", n) for n in range(VOLT_CHUNKS)]
        for t in range(IM_TILES):
            load_order.extend([("im", t * IM_CHUNKS + c) for c in range(IM_CHUNKS)])
            if t >= FIRST_YBR_TILE:
                load_order.append(("ybr", t - FIRST_YBR_TILE))
        used = {}
        raw = {}

        def value_of_tile(t):
            return 2 * (t % 2) + t % PACK // 2

        def load(kind, n):
            if kind == "volt":
                tile = raw_pool.tile([P, SAMPLE_TILES, volt_chunk_k], BF16, tag="raw")
                source = volt_rows[:, :, n * volt_chunk_k : (n + 1) * volt_chunk_k]
            elif kind == "im":
                tile = raw_pool.tile([P, im_chunk_k], BF16, tag="raw")
                t, c = n // IM_CHUNKS, n % IM_CHUNKS
                source = im_rows[t // PACK, value_of_tile(t), :, c * im_chunk_k : (c + 1) * im_chunk_k]
            else:
                tile = raw_pool.tile([P, 2 * CURRENTS], BF16, tag="raw")
                source = ybr_rows[n]
            nc.sync.dma_start(out=tile[:], in_=source)
            raw[(kind, n)] = tile

        def mark_used(kind, n):
            used[(kind, n)] = True
            while len(raw) < len(load_order) and load_order[len(raw) - RAW_TILES] in used:
                load(*load_order[len(raw)])

        def sort_words(chunk):
            passes = IM_CHUNK_PASSES
            tile = sorted_pool.tile([P, passes, 2, P], F32, tag="sorted", name="sorted_words")
            nc.vector.tensor_copy(
                out=tile[:],
                in_=raw[("im", chunk)][:].bitcast(F32).rearrange("p (a w h) -> p a h w", a=passes, h=2),
            )
            return tile

        def transpose_banks(words):
            grouped = grouped_pool.tile([P, len(words), 2 * P * PACK], BF16, tag="grouped", align_bytes=64)
            for bank in range(len(words)):
                flipped = bank_pool.tile([P, 2, 2, P], F32, tag="bank")
                for s in range(2):
                    for h in range(2):
                        nc.tensor.transpose(flipped[:, s, h, :], words[bank][:, s, h, :], identity[:])
                pairs_out = grouped[:, bank, :].bitcast(F32).rearrange("p (s r h) -> p s r h", s=2, h=2)
                pairs_in = flipped[:].rearrange("p s h r -> p s r h")
                nc.scalar.copy(out=pairs_out, in_=pairs_in)
            return grouped

        def quantise(grouped, codes, scales):
            nc.vector.quantize_mx(out=codes.bitcast(FP8X4), scales=scales, in_=grouped)

        for item in load_order[:RAW_TILES]:
            load(*item)

        waiting = []

        def quantise_waiting():
            for operands in waiting:
                quantise(*operands)
            waiting.clear()

        in_order = {}

        def sort_up_to(last):
            for chunk in range(min(last + 1, IM_TILES * IM_CHUNKS)):
                if chunk not in in_order:
                    in_order[chunk] = sort_words(chunk)
                    mark_used("im", chunk)

        def transpose_volt(c):
            words = raw[("volt", c)][:].bitcast(F32).rearrange("p s (b w h) -> p b s h w", b=VOLT_CHUNK_PASSES, h=2)
            quantise_waiting()
            sort_up_to(c - VOLT_CHUNKS + 1)
            grouped = transpose_banks([words[:, b] for b in range(VOLT_CHUNK_PASSES)])
            mark_used("volt", c)
            passes = slice(c * VOLT_CHUNK_PASSES, (c + 1) * VOLT_CHUNK_PASSES)
            waiting.append(
                (
                    grouped[:].rearrange("p b v -> p (b v)"),
                    volt_codes[:, passes, :].rearrange("p a r -> p (a r)"),
                    volt_scales[:, passes, :].rearrange("p a r -> p (a r)"),
                )
            )

        im_tiles = {}

        def transpose_im(t, c):
            if t not in im_tiles:
                im_codes = im_pool.tile([P, PASSES_1, P], U32, align_bytes=64)
                im_scales = im_pool.tile([P, PASSES_1, P], U8, align_bytes=64)
                im_tiles[t] = (im_codes, im_scales)
            im_codes, im_scales = im_tiles[t]
            chunk = t * IM_CHUNKS + c
            sort_up_to(chunk + 1)
            quantise_waiting()
            words = in_order[chunk][:].rearrange("p (b s) h w -> p b s h w", s=2)
            grouped = transpose_banks([words[:, b] for b in range(IM_CHUNK_PASSES // 2)])
            passes = slice(c * IM_CHUNK_PASSES, (c + 1) * IM_CHUNK_PASSES)
            waiting.append(
                (
                    grouped[:].rearrange("p b v -> p (b v)"),
                    im_codes[:, passes, :].rearrange("p a r -> p (a r)"),
                    im_scales[:, passes, :].rearrange("p a r -> p (a r)"),
                )
            )

        def transpose_ybr(unit):
            words = raw[("ybr", unit)][:].bitcast(F32).rearrange("p (s g w h) -> p g s h w", s=2, g=PASSES_2, h=2)
            grouped = transpose_banks([words[:, g] for g in range(PASSES_2)])
            mark_used("ybr", unit)
            part, q = unit // LINE_BLOCKS, unit % LINE_BLOCKS
            for g in range(PASSES_2):
                waiting.append((grouped[:, g, :], ybr_codes[:, g, q, part, :], ybr_scales[:, g, q, part, :]))

        dv_banks = {}

        def first_matmul(t, chunks):
            im_codes, im_scales = im_tiles[t]
            bank = (t // PACK, t % 2)
            if bank not in dv_banks:
                dv_banks[bank] = acc_pool.tile([P, 2, SAMPLES], F32, tag="acc", name="acc")
            for a in range(chunks[0] * IM_CHUNK_PASSES, (chunks[-1] + 1) * IM_CHUNK_PASSES):
                nc.tensor.matmul_mx(
                    out=dv_banks[bank][:, t % PACK // 2, :],
                    lhsT=im_codes[:, a, :].bitcast(FP8X4),
                    lhsT_scale=im_scales[:, a, :],
                    rhs=volt_codes[:, a, :].bitcast(FP8X4),
                    rhs_scale=volt_scales[:, a, :],
                    start=(a == 0),
                    stop=(a == PASSES_1 - 1),
                )

        def round_dv(g, b):
            nc.vector.tensor_copy(
                out=dv_grouped[:, g, :, 2 * b : 2 * b + 2], in_=dv_banks[(g, b)][:].rearrange("p e n -> p n e")
            )
            if b == 1:
                quantise(dv_grouped[:, g].rearrange("p n v -> p (n v)"), dv_codes[:, g, :], dv_scales[:, g, :])

        for c in range(VOLT_CHUNKS):
            transpose_volt(c)

        complete = []

        multiplied = []

        def multiply(last):
            for chunk in range(len(multiplied), last + 1):
                t, c = chunk // IM_CHUNKS, chunk % IM_CHUNKS
                first_matmul(t, [c])
                multiplied.append(chunk)
                if c == IM_CHUNKS - 1 and t % PACK >= 2:
                    complete.append((t // PACK, t % 2))

        for chunk in range(IM_TILES * IM_CHUNKS):
            t, c = chunk // IM_CHUNKS, chunk % IM_CHUNKS
            transpose_im(t, c)
            if complete:
                round_dv(*complete[0])
                complete.clear()
            if c == IM_CHUNKS - 1 and t >= FIRST_YBR_TILE:
                transpose_ybr(t - FIRST_YBR_TILE)
            if c == 0 and t == IM_TILES - 2:
                nc.sync.dma_start(out=mu[:], in_=n_o_mu_i_u.rearrange("(t p) l -> p t l", p=P))
            multiply(chunk - 2)
        multiply(IM_TILES * IM_CHUNKS - 2)
        quantise_waiting()
        multiply(IM_TILES * IM_CHUNKS - 1)
        round_dv(PASSES_2 - 1, 0)

        ibr = {}

        def second_matmul(q, t, passes):
            samples = slice(t * P, (t + 1) * P)
            if (q, t) not in ibr:
                ibr[(q, t)] = bank_pool.tile([P, 2 * BANK_COLS], F32, tag="bank", name="ibr")
            for g in passes:
                nc.tensor.matmul_mx(
                    out=ibr[(q, t)][:],
                    lhsT=dv_codes[:, g, samples].bitcast(FP8X4),
                    lhsT_scale=dv_scales[:, g, samples],
                    rhs=ybr_codes[:, g, q].rearrange("p c n -> p (c n)").bitcast(FP8X4),
                    rhs_scale=ybr_scales[:, g, q].rearrange("p c n -> p (c n)"),
                    start=(g == 0),
                    stop=(g == PASSES_2 - 1),
                )

        blocks = [(q, t) for q in range(LINE_BLOCKS) for t in range(SAMPLE_TILES)]
        for q, t in blocks[:EARLY_BLOCKS]:
            second_matmul(q, t, range(PASSES_2 - 1))
        round_dv(PASSES_2 - 1, 1)
        for s in range(SAMPLE_TILES):
            negative_part = work.tile([P, LINES], F32)
            nc.scalar.activation(
                out=negative_part[:], in_=mu[:, s, :], func=ACT.Relu, scale=-2.0,
                accum_out=terms[:, s, 0, LINE_BLOCKS : LINE_BLOCKS + 1],
            )
            mu_size = work.tile([P, LINES], F32)
            nc.scalar.activation(out=mu_size[:], in_=mu[:, s, :], func=ACT.Abs)
            nc.vector.tensor_scalar(
                out=weight[:, s, :], in0=mu_size[:], scalar1=2.0, scalar2=1.0, op0=ALU.mult, op1=ALU.add
            )

        def weighted_sum(q, t, i_up):
            i_size = sums.tile([P, BANK_COLS], F32)
            nc.scalar.activation(out=i_size[:], in_=i_up[:], func=ACT.Abs)
            weighted = sums.tile([P, BANK_COLS], F32)
            nc.vector.scalar_tensor_tensor(
                out=weighted[:].rearrange("p (s r) -> p s r", s=2),
                in0=i_size[:].rearrange("p (s r) -> p s r", s=2),
                scalar=1.0,
                in1=weight[:, t, q * BANK_COLS : (q + 1) * BANK_COLS].rearrange("p (r s) -> p s r", s=2),
                op0=ALU.mult, op1=ALU.mult, accum_out=terms[:, t, 1, q : q + 1],
            )

        not_summed = []
        for q, t in blocks:
            second_matmul(q, t, range(PASSES_2 - 1 if (q, t) in ibr else 0, PASSES_2))
            squares = sums.tile([P, 2, BANK_COLS], F32)
            nc.scalar.activation(
                out=squares[:].rearrange("p c n -> p (c n)"), in_=ibr[(q, t)][:], func=ACT.Square,
                accum_out=terms[:, t, 0, q : q + 1],
            )
            i_up = sums.tile([P, BANK_COLS], F32)
            nc.vector.scalar_tensor_tensor(
                out=i_up[:], in0=squares[:, 0, :], scalar=-LIMIT_SQUARED, in1=squares[:, 1, :],
                op0=ALU.add, op1=ALU.add,
            )
            not_summed.append((q, t, i_up))
            if len(not_summed) > 3:
                weighted_sum(*not_summed[0])
                not_summed.remove(not_summed[0])
        for block in not_summed:
            weighted_sum(*block)

        nc.vector.tensor_reduce(
            out=totals[:, 0:SAMPLE_TILES], in_=terms[:].rearrange("p t w c -> p t (w c)"),
            axis=mybir.AxisListType.X, op=ALU.add,
        )
        totals_flipped = acc_pool.tile([P, P], F32, tag="acc")
        nc.tensor.transpose(totals_flipped[:], totals[:], identity[:])
        rows = keep.tile([P, P], F32)
        nc.vector.tensor_scalar(
            out=rows[:], in0=totals_flipped[:], scalar1=0.5, scalar2=-0.5 * LINES * LIMIT_SQUARED,
            op0=ALU.mult, op1=ALU.add,
        )
        nc.sync.dma_start(out=out.rearrange("(t b) -> t b", t=SAMPLE_TILES), in_=rows[0:SAMPLE_TILES, :])
